import numpy as np
import ml_dtypes


def mxq(x, axis, fmt="e4m3"):
    dtype, down = {"e4m3": (ml_dtypes.float8_e4m3fn, 7), "e5m2": (ml_dtypes.float8_e5m2, 14)}[fmt]
    v = np.moveaxis(np.asarray(x, np.float32).astype(ml_dtypes.bfloat16).astype(np.float64), axis, -1)
    blocks = v.reshape(v.shape[:-1] + (-1, 32))
    amax = np.abs(blocks).max(-1, keepdims=True)
    byte = np.maximum(np.where(amax > 0, np.frexp(amax)[1] - 1 + 127, 0) - down, 1)
    scale = np.exp2(byte - 127.0)
    codes = (blocks / scale).astype(np.float32).astype(dtype).astype(np.float64)
    return np.moveaxis((codes * scale).reshape(v.shape), -1, axis)


WIDE = False


def mx_kscale(k):
    if not WIDE:
        return np.ones(k)
    levels = np.array([10, -10, 5, -5, 0])
    a = np.random.permutation(np.resize(levels, k // 512 * 4)).reshape(k // 512, 4)
    idx = np.arange(k)
    return np.exp2(a[idx // 512, idx % 128 // 32])


BF16 = ml_dtypes.bfloat16


def bf(x):
    return np.asarray(x, np.float32).astype(BF16)


def f64(x):
    return np.asarray(x).astype(np.float64)


E2M1 = np.array([0.0, 0.5, 1.0, 1.5, 2.0, 3.0, 4.0, 6.0, -0.0, -0.5, -1.0, -1.5, -2.0, -3.0, -4.0, -6.0])


def pack_weight(w, fmt):
    k, n = w.shape
    w = f64(bf(w)).reshape(k // 32, 32, n)
    amax = np.abs(w).max(1)
    if fmt == "e4m3":
        byte = np.frexp(amax)[1] - 1 + 127 - 7
    else:
        mant, ex = np.frexp(amax / 6.0)
        byte = np.where(mant > 0.5, ex, ex - 1) + 127
    byte = np.clip(np.where(amax > 0, byte, 1), 1, 254)
    scaled = (w * np.exp2(127.0 - byte)[:, None, :]).reshape(k, n).astype(np.float32)
    by_word = np.ascontiguousarray(scaled.reshape(k // 512, 128, 4, n).transpose(0, 1, 3, 2))
    if fmt == "e4m3":
        words = by_word.astype(ml_dtypes.float8_e4m3fn).view(np.uint8)
    else:
        c = by_word.astype(ml_dtypes.float4_e2m1fn).view(np.uint8) & 0xF
        words = c[..., 0::2] | (c[..., 1::2] << 4)
    return np.ascontiguousarray(words), np.ascontiguousarray(byte.astype(np.uint8).reshape(k // 512, 16, n))


def unpack_weight(words, scales, fmt):
    g, p, n, _ = words.shape
    if fmt == "e4m3":
        vals = np.ascontiguousarray(words).view(ml_dtypes.float8_e4m3fn).astype(np.float64)
    else:
        nib = np.empty((g, p, n, 4), np.uint8)
        nib[..., 0::2] = words & 0xF
        nib[..., 1::2] = words >> 4
        vals = E2M1[nib]
    vals = vals * np.repeat(np.exp2(scales.astype(np.float64) - 127.0), 8, axis=1)[..., None]
    return vals.transpose(0, 1, 3, 2).reshape(g * 512, n)

def pack4(w):
    words, scales = pack_weight(w, "e2m1")
    return words.reshape(words.shape[0], 128, -1), scales


def unpack4(words, scales):
    return unpack_weight(words.reshape(words.shape[0], 128, -1, 2), scales, "e2m1")


B, T, D, O = 128, 32, 512, 512


def erf(z):
    a = np.clip(z, -6.0, 6.0)
    q = 2.0 * a * a
    term = a.copy()
    total = a.copy()
    for k in range(1, 130):
        term = term * q / (2 * k + 1)
        total = total + term
    return 2.0 / np.sqrt(np.pi) * np.exp(-a * a) * total


def gelu_exact(v):
    return 0.5 * v * (1.0 + erf(v / np.sqrt(2.0)))


def setup_inputs():
    s = mx_kscale(D)
    x = np.random.standard_normal((B, T, D)) * s
    lengths = np.random.randint(T // 4, T + 1, size=B)
    lengths[np.random.randint(B)] = T
    pad = np.arange(T)[None, :] >= lengths[:, None]
    x = np.where(pad[:, :, None], -1.0, x)
    w = np.random.standard_normal((O, D)) / np.sqrt(D) / s[None, :]
    words, scales = pack4(np.ascontiguousarray(w.T))
    return {"x": bf(x), "W_words": words, "W_scales": scales, "b": bf(np.random.standard_normal(O) * 0.3)}


def reference(x, W_words, W_scales, b):
    x = f64(x)
    valid = ~np.all(x == -1.0, axis=-1)
    y = gelu_exact((mxq(x, 2, "e4m3") @ unpack4(W_words, W_scales)) + f64(b))
    vf = valid[..., None].astype(np.float64)
    n = np.sum(vf, axis=1)
    mean = np.sum(y * vf, axis=1) / n
    diff = (y - mean[:, None, :]) * vf
    var = np.sum(diff * diff, axis=1) / np.maximum(n - 1.0, 1.0)
    std = np.where(n > 1.0, np.sqrt(var), np.zeros_like(var))
    out = np.concatenate([std, mean], axis=-1)
    return np.where(np.isnan(out), np.zeros_like(out), out)

@@ -1,0 +1,247 @@
+from contextlib import ExitStack
+
+import concourse.mybir as mybir
+from concourse.masks import make_identity
+
+F32 = mybir.dt.float32
+BF16 = mybir.dt.bfloat16
+I32 = mybir.dt.int32
+U32 = mybir.dt.uint32
+U8 = mybir.dt.uint8
+FP8X4 = mybir.dt.float8_e4m3fn_x4
+FP4X4 = mybir.dt.float4_e2m1fn_x4
+ALU = mybir.AluOpType
+ACT = mybir.ActivationFunctionType
+
+P = 128
+SAMPLES = 128
+TOKENS = 32
+K = 512
+OUT = 512
+CHUNKS = OUT // P
+BLOCK = 512
+TILES = BLOCK // P
+NBLOCKS = SAMPLES * TOKENS // BLOCK
+BLOCK_SAMPLES = BLOCK // TOKENS
+WORDS = K // 2
+MINUS_PAD_WORD = 1.0 + 0xBF80 / 2.0**23
+
+FLOPS = 2 * SAMPLES * TOKENS * K * OUT
+
+
+def tile_linearnnencoder_kernel(tc, x, W_words, W_scales, b, out):
+    nc = tc.nc
+    x_rows = x.rearrange("s t k -> (s t) k")
+
+    with ExitStack() as ctx:
+        const = ctx.enter_context(tc.tile_pool(name="const", bufs=1))
+        x_pool = ctx.enter_context(tc.tile_pool(name="x_pool", bufs=NBLOCKS))
+        work = ctx.enter_context(tc.tile_pool(name="work", bufs=3))
+        y_pool = ctx.enter_context(tc.tile_pool(name="y_pool", bufs=6))
+        flip_psum = ctx.enter_context(tc.psum_pool(name="flip_psum", bufs=4))
+        acc_psum = ctx.enter_context(tc.psum_pool(name="acc_psum", bufs=4))
+
+        x_blocks = []
+        for blk in range(NBLOCKS):
+            x_blk = x_pool.tile([P, TILES, K], BF16, name="x_blk")
+            x_blocks.append(x_blk)
+
+        def load_x(blk):
+            nc.sync.dma_start(
+                out=x_blocks[blk][:],
+                in_=x_rows[blk * BLOCK : (blk + 1) * BLOCK, :].rearrange("(i p) k -> p i k", p=P),
+            )
+
+        w_words = const.tile([P, 2 * OUT], U8, align_bytes=64)
+        w_scales = const.tile([P, OUT], U8, align_bytes=64)
+        b_rows = const.tile([P, OUT], BF16)
+        nc.vector.memset(w_scales[:].bitcast(I32), 0)
+        nc.scalar.dma_start(out=b_rows[:], in_=b.partition_broadcast(P))
+        load_x(0)
+        nc.sync.dma_start(out=w_words[:].bitcast(I32), in_=W_words[0].bitcast(I32))
+        for quad in range(4):
+            nc.sync.dma_start(
+                out=w_scales[32 * quad : 32 * quad + 4, :].bitcast(I32),
+                in_=W_scales[0, 4 * quad : 4 * quad + 4, :].bitcast(I32),
+            )
+        for blk in range(1, NBLOCKS):
+            load_x(blk)
+
+        ident = const.tile([P, P], F32)
+        make_identity(nc, ident[:])
+        minus_pad_word = const.tile([P, 1], F32)
+        nc.vector.memset(minus_pad_word[:], MINUS_PAD_WORD)
+        ones = const.tile([P, 32], BF16)
+        nc.vector.memset(ones[:], 1.0)
+        quadrant = const.tile([P, 4], F32)
+        nc.vector.memset(quadrant[:], 0.0)
+        for quad in range(4):
+            nc.vector.memset(quadrant[32 * quad : 32 * quad + 32, quad : quad + 1], 1.0)
+
+        b_f32 = const.tile([P, OUT], F32)
+        nc.vector.tensor_copy(out=b_f32[:], in_=b_rows[:])
+        b_ps = acc_psum.tile([P, CHUNKS, P], F32, tag="acc")
+        for c in range(CHUNKS):
+            nc.tensor.transpose(b_ps[:, c, :], b_f32[:, c * P : (c + 1) * P], ident[:])
+        b_col = const.tile([P, CHUNKS], F32)
+        nc.vector.tensor_copy(out=b_col[:], in_=b_ps[:, :, 0])
+        pad_y_rows = const.tile([P, OUT], F32)
+        nc.scalar.activation(out=pad_y_rows[:], in_=b_rows[:], func=ACT.Gelu)
+        pad_y_col = const.tile([P, CHUNKS], F32)
+        nc.scalar.activation(out=pad_y_col[:], in_=b_col[:], func=ACT.Gelu)
+
+        distance = const.tile([P, NBLOCKS * TILES], F32)
+        junk = const.tile([P, WORDS], F32)
+        stats = const.tile([P, CHUNKS, SAMPLES, 3], F32)
+
+        row_masks = {}
+        codes = {}
+
+        def test_rows(blk):
+            for i in range(TILES):
+                t = blk * TILES + i
+                nc.scalar.activation(
+                    out=junk[:],
+                    in_=x_blocks[blk][:, i, :].bitcast(F32),
+                    func=ACT.Square,
+                    bias=minus_pad_word[:, 0:1],
+                    accum_out=distance[:, t : t + 1],
+                )
+
+        def make_masks(blk):
+            mask = work.tile([P, TILES, P], F32, name="mask")
+            for i in range(TILES):
+                t = blk * TILES + i
+                nc.vector.tensor_scalar(
+                    out=mask[:, i, :],
+                    in0=ident[:],
+                    scalar1=distance[:, t : t + 1],
+                    scalar2=0.0,
+                    op0=ALU.mult,
+                    op1=ALU.is_gt,
+                )
+            row_masks[blk] = mask
+
+        def flip(blk):
+            x_words = x_blocks[blk][:].bitcast(F32)
+            grouped = work.tile([P, 4 * BLOCK], BF16, name="grouped", align_bytes=64)
+            grouped_words = grouped[:].bitcast(F32)
+            for half in range(2):
+                planes = flip_psum.tile([P, 2, 2 * P], F32, name="planes")
+                for j in range(2):
+                    i = 2 * half + j
+                    for u in range(2):
+                        nc.tensor.transpose(
+                            planes[:, u, j * P : (j + 1) * P],
+                            x_words[:, i, u:WORDS:2],
+                            row_masks[blk][:, i, :],
+                        )
+                dst = grouped_words[:, half * BLOCK : (half + 1) * BLOCK].rearrange("p (r u) -> p r u", u=2)
+                src = planes[:].rearrange("p u r -> p r u")
+                if half == 0:
+                    nc.scalar.copy(out=dst, in_=src)
+                else:
+                    nc.vector.tensor_copy(out=dst, in_=src)
+            x_codes = work.tile([P, BLOCK], U32, name="x_codes", align_bytes=64)
+            x_scales = work.tile([P, BLOCK], U8, name="x_scales", align_bytes=64)
+            nc.vector.quantize_mx(out=x_codes[:].bitcast(FP8X4), scales=x_scales[:], in_=grouped[:])
+            codes[blk] = (x_codes, x_scales)
+
+        def layer(blk):
+            x_codes, x_scales = codes[blk]
+            for c in range(CHUNKS):
+                acc = acc_psum.tile([P, BLOCK], F32, name="acc")
+                nc.tensor.matmul_mx(
+                    out=acc[:],
+                    lhsT=w_words[:, 2 * c * P : 2 * (c + 1) * P].bitcast(FP4X4),
+                    lhsT_scale=w_scales[:, c * P : (c + 1) * P],
+                    rhs=x_codes[:].bitcast(FP8X4),
+                    rhs_scale=x_scales[:],
+                    start=True,
+                    stop=True,
+                )
+                y = y_pool.tile([P, BLOCK], F32, name="y")
+                nc.scalar.activation(out=y[:], in_=acc[:], func=ACT.Gelu, bias=b_col[:, c : c + 1])
+                for pair in range(BLOCK_SAMPLES // 2):
+                    s = blk * BLOCK_SAMPLES + 2 * pair
+                    nc.vector.bn_stats(
+                        out=stats[:, c, s : s + 2, :].rearrange("p s v -> p (s v)"),
+                        in_=y[:, 2 * pair * TOKENS : 2 * (pair + 1) * TOKENS].rearrange("p (s t) -> p t s", s=2),
+                    )
+
+        test_rows(0)
+        make_masks(0)
+        test_rows(1)
+        make_masks(1)
+        flip(0)
+        for blk in range(NBLOCKS):
+            if blk + 1 < NBLOCKS:
+                flip(blk + 1)
+            if blk + 2 < NBLOCKS:
+                test_rows(blk + 2)
+                make_masks(blk + 2)
+            layer(blk)
+
+        valid = const.tile([P, NBLOCKS * TILES], F32)
+        nc.vector.tensor_single_scalar(out=valid[:], in_=distance[:], scalar=0.0, op=ALU.is_gt)
+        spread = const.tile([P, NBLOCKS * TILES, 4], BF16)
+        nc.vector.tensor_tensor(
+            out=spread[:],
+            in0=valid[:].unsqueeze(2).to_broadcast([P, NBLOCKS * TILES, 4]),
+            in1=quadrant[:].unsqueeze(1).to_broadcast([P, NBLOCKS * TILES, 4]),
+            op=ALU.mult,
+        )
+        n_ps = flip_psum.tile([P, 32], F32, tag="planes")
+        nc.tensor.matmul(out=n_ps[:], lhsT=spread[:].rearrange("p i q -> p (i q)"), rhs=ones[:], start=True, stop=True)
+        n = const.tile([P, 1], F32)
+        nc.vector.tensor_copy(out=n[:], in_=n_ps[:, 0:1])
+        inv_n = const.tile([P, 1], F32)
+        nc.vector.tensor_scalar_max(out=inv_n[:], in0=n[:], scalar1=1.0)
+        nc.vector.reciprocal(out=inv_n[:], in_=inv_n[:])
+        some = const.tile([P, 1], F32)
+        nc.vector.tensor_scalar_min(out=some[:], in0=n[:], scalar1=1.0)
+        stretch = const.tile([P, 1], F32)
+        nc.vector.tensor_scalar(
+            out=stretch[:], in0=inv_n[:], scalar1=float(TOKENS), scalar2=some[:, 0:1], op0=ALU.mult, op1=ALU.mult
+        )
+        between = const.tile([P, 1], F32)
+        nc.vector.tensor_scalar(
+            out=between[:], in0=n[:], scalar1=-float(TOKENS), scalar2=float(TOKENS), op0=ALU.add, op1=ALU.mult
+        )
+        nc.vector.tensor_mul(out=between[:], in0=between[:], in1=inv_n[:])
+        inv_dof = const.tile([P, 1], F32)
+        nc.vector.tensor_scalar(out=inv_dof[:], in0=n[:], scalar1=-1.0, scalar2=1.0, op0=ALU.add, op1=ALU.max)
+        nc.vector.reciprocal(out=inv_dof[:], in_=inv_dof[:])
+        scale_var = const.tile([P, 1], F32)
+        nc.vector.tensor_scalar(
+            out=scale_var[:], in0=n[:], scalar1=1.0, scalar2=inv_dof[:, 0:1], op0=ALU.is_gt, op1=ALU.mult
+        )
+        pad_y_some = const.tile([P, OUT], F32)
+        nc.vector.tensor_scalar_mul(out=pad_y_some[:], in0=pad_y_rows[:], scalar1=some[:, 0:1])
+
+        shift = const.tile([P, CHUNKS, SAMPLES], F32)
+        m32 = const.tile([P, CHUNKS, SAMPLES], F32)
+        shift_t = acc_psum.tile([P, OUT], F32, tag="acc")
+        m32_t = acc_psum.tile([P, OUT], F32, tag="acc")
+        for c in range(CHUNKS):
+            nc.vector.tensor_scalar(
+                out=shift[:, c, :], in0=stats[:, c, :, 1], scalar1=pad_y_col[:, c : c + 1], scalar2=None, op0=ALU.subtract
+            )
+            nc.tensor.transpose(shift_t[:, c * P : (c + 1) * P], shift[:, c, :], ident[:])
+        for c in range(CHUNKS):
+            nc.vector.tensor_copy(out=m32[:, c, :], in_=stats[:, c, :, 2])
+            nc.tensor.transpose(m32_t[:, c * P : (c + 1) * P], m32[:, c, :], ident[:])
+        result = const.tile([P, 2 * OUT], F32)
+        square = const.tile([P, OUT], F32)
+        nc.scalar.activation(out=square[:], in_=shift_t[:], func=ACT.Square)
+        nc.vector.scalar_tensor_tensor(
+            out=result[:, OUT : 2 * OUT], in0=shift_t[:], scalar=stretch[:, 0:1], in1=pad_y_some[:], op0=ALU.mult, op1=ALU.add
+        )
+        nc.sync.dma_start(out=out[:, OUT : 2 * OUT], in_=result[:, OUT : 2 * OUT])
+        within = const.tile([P, OUT], F32)
+        nc.vector.scalar_tensor_tensor(
+            out=within[:], in0=square[:], scalar=between[:, 0:1], in1=m32_t[:], op0=ALU.mult, op1=ALU.add
+        )
+        nc.vector.tensor_scalar_max(out=within[:], in0=within[:], scalar1=0.0)
+        nc.scalar.activation(out=result[:, 0:OUT], in_=within[:], func=ACT.Sqrt, scale=scale_var[:, 0:1])
+        nc.sync.dma_start(out=out[:, 0:OUT], in_=result[:, 0:OUT])

@@ -22,6 +22,7 @@ CHUNKS = OUT // P
 BLOCK = 512
 TILES = BLOCK // P
 NBLOCKS = SAMPLES * TOKENS // BLOCK
+NTILES = NBLOCKS * TILES
 BLOCK_SAMPLES = BLOCK // TOKENS
 WORDS = K // 2
 MINUS_PAD_WORD = 1.0 + 0xBF80 / 2.0**23
@@ -40,24 +41,21 @@ def tile_linearnnencoder_kernel(tc, x, W_words, W_scales, b, out):
         y_pool = ctx.enter_context(tc.tile_pool(name="y_pool", bufs=6))
         flip_psum = ctx.enter_context(tc.psum_pool(name="flip_psum", bufs=4))
         acc_psum = ctx.enter_context(tc.psum_pool(name="acc_psum", bufs=4))
+        ctx.enter_context(tc.manual_schedule())
 
         x_blocks = []
         for blk in range(NBLOCKS):
             x_blk = x_pool.tile([P, TILES, K], BF16, name="x_blk")
             x_blocks.append(x_blk)
 
-        def load_x(blk):
-            nc.sync.dma_start(
-                out=x_blocks[blk][:],
-                in_=x_rows[blk * BLOCK : (blk + 1) * BLOCK, :].rearrange("(i p) k -> p i k", p=P),
-            )
-
         w_words = const.tile([P, 2 * OUT], U8, align_bytes=64)
         w_scales = const.tile([P, OUT], U8, align_bytes=64)
-        b_rows = const.tile([P, OUT], BF16)
+        b_top = const.tile([P, P], BF16)
         nc.vector.memset(w_scales[:].bitcast(I32), 0)
-        nc.scalar.dma_start(out=b_rows[:], in_=b.partition_broadcast(P))
-        load_x(0)
+        nc.vector.memset(b_top[:], 0.0)
+        nc.scalar.dma_start(out=b_top[0:CHUNKS, :], in_=b.rearrange("(c f) -> c f", f=P))
+        for i in range(TILES):
+            nc.sync.dma_start(out=x_blocks[0][:, i, :], in_=x_rows[i * P : (i + 1) * P, :])
         nc.sync.dma_start(out=w_words[:].bitcast(I32), in_=W_words[0].bitcast(I32))
         for quad in range(4):
             nc.sync.dma_start(
@@ -65,10 +63,17 @@ def tile_linearnnencoder_kernel(tc, x, W_words, W_scales, b, out):
                 in_=W_scales[0, 4 * quad : 4 * quad + 4, :].bitcast(I32),
             )
         for blk in range(1, NBLOCKS):
-            load_x(blk)
+            nc.sync.dma_start(
+                out=x_blocks[blk][:],
+                in_=x_rows[blk * BLOCK : (blk + 1) * BLOCK, :].rearrange("(i p) k -> p i k", p=P),
+            )
 
         ident = const.tile([P, P], F32)
         make_identity(nc, ident[:])
+        one = const.tile([P, 1], F32)
+        nc.vector.memset(one[:], 1.0)
+        warm = const.tile([P, 1], F32)
+        nc.scalar.activation(out=warm[:], in_=one[:], func=ACT.Gelu)
         minus_pad_word = const.tile([P, 1], F32)
         nc.vector.memset(minus_pad_word[:], MINUS_PAD_WORD)
         ones = const.tile([P, 32], BF16)
@@ -77,20 +82,15 @@ def tile_linearnnencoder_kernel(tc, x, W_words, W_scales, b, out):
         nc.vector.memset(quadrant[:], 0.0)
         for quad in range(4):
             nc.vector.memset(quadrant[32 * quad : 32 * quad + 32, quad : quad + 1], 1.0)
+        ident_bf = const.tile([P, 32], BF16)
+        nc.vector.tensor_copy(out=ident_bf[:], in_=ident[:, 0:32])
 
-        b_f32 = const.tile([P, OUT], F32)
-        nc.vector.tensor_copy(out=b_f32[:], in_=b_rows[:])
-        b_ps = acc_psum.tile([P, CHUNKS, P], F32, tag="acc")
-        for c in range(CHUNKS):
-            nc.tensor.transpose(b_ps[:, c, :], b_f32[:, c * P : (c + 1) * P], ident[:])
+        b_ps = acc_psum.tile([P, 32], F32, tag="acc")
+        nc.tensor.matmul(out=b_ps[:], lhsT=b_top[:], rhs=ident_bf[:], start=True, stop=True)
         b_col = const.tile([P, CHUNKS], F32)
-        nc.vector.tensor_copy(out=b_col[:], in_=b_ps[:, :, 0])
-        pad_y_rows = const.tile([P, OUT], F32)
-        nc.scalar.activation(out=pad_y_rows[:], in_=b_rows[:], func=ACT.Gelu)
-        pad_y_col = const.tile([P, CHUNKS], F32)
-        nc.scalar.activation(out=pad_y_col[:], in_=b_col[:], func=ACT.Gelu)
+        nc.vector.tensor_copy(out=b_col[:], in_=b_ps[:, 0:CHUNKS])
 
-        distance = const.tile([P, NBLOCKS * TILES], F32)
+        distance = const.tile([P, NTILES], F32)
         junk = const.tile([P, WORDS], F32)
         stats = const.tile([P, CHUNKS, SAMPLES, 3], F32)
 
@@ -107,8 +107,6 @@ def tile_linearnnencoder_kernel(tc, x, W_words, W_scales, b, out):
                     bias=minus_pad_word[:, 0:1],
                     accum_out=distance[:, t : t + 1],
                 )
-
-        def make_masks(blk):
             mask = work.tile([P, TILES, P], F32, name="mask")
             for i in range(TILES):
                 t = blk * TILES + i
@@ -136,19 +134,18 @@ def tile_linearnnencoder_kernel(tc, x, W_words, W_scales, b, out):
                             x_words[:, i, u:WORDS:2],
                             row_masks[blk][:, i, :],
                         )
-                dst = grouped_words[:, half * BLOCK : (half + 1) * BLOCK].rearrange("p (r u) -> p r u", u=2)
-                src = planes[:].rearrange("p u r -> p r u")
-                if half == 0:
-                    nc.scalar.copy(out=dst, in_=src)
-                else:
-                    nc.vector.tensor_copy(out=dst, in_=src)
+                nc.scalar.copy(
+                    out=grouped_words[:, half * BLOCK : (half + 1) * BLOCK].rearrange("p (r u) -> p r u", u=2),
+                    in_=planes[:].rearrange("p u r -> p r u"),
+                )
             x_codes = work.tile([P, BLOCK], U32, name="x_codes", align_bytes=64)
             x_scales = work.tile([P, BLOCK], U8, name="x_scales", align_bytes=64)
             nc.vector.quantize_mx(out=x_codes[:].bitcast(FP8X4), scales=x_scales[:], in_=grouped[:])
             codes[blk] = (x_codes, x_scales)
 
-        def layer(blk):
+        def layer(blk, after_chunk):
             x_codes, x_scales = codes[blk]
+            accs = []
             for c in range(CHUNKS):
                 acc = acc_psum.tile([P, BLOCK], F32, name="acc")
                 nc.tensor.matmul_mx(
@@ -160,88 +157,128 @@ def tile_linearnnencoder_kernel(tc, x, W_words, W_scales, b, out):
                     start=True,
                     stop=True,
                 )
+                accs.append(acc)
+            for c in range(CHUNKS):
                 y = y_pool.tile([P, BLOCK], F32, name="y")
-                nc.scalar.activation(out=y[:], in_=acc[:], func=ACT.Gelu, bias=b_col[:, c : c + 1])
+                nc.scalar.activation(out=y[:], in_=accs[c][:], func=ACT.Gelu, bias=b_col[:, c : c + 1])
                 for pair in range(BLOCK_SAMPLES // 2):
                     s = blk * BLOCK_SAMPLES + 2 * pair
                     nc.vector.bn_stats(
                         out=stats[:, c, s : s + 2, :].rearrange("p s v -> p (s v)"),
                         in_=y[:, 2 * pair * TOKENS : 2 * (pair + 1) * TOKENS].rearrange("p (s t) -> p t s", s=2),
                     )
+                after_chunk(c)
+
+        def nothing(c):
+            return None
+
+        spread = const.tile([P, NTILES, 4], BF16)
+        pad_y_col = const.tile([P, CHUNKS], F32)
+
+        def mark_valid_rows():
+            valid = const.tile([P, NTILES], F32)
+            nc.vector.tensor_single_scalar(out=valid[:], in_=distance[:], scalar=0.0, op=ALU.is_gt)
+            nc.vector.tensor_tensor(
+                out=spread[:],
+                in0=valid[:].unsqueeze(2).to_broadcast([P, NTILES, 4]),
+                in1=quadrant[:].unsqueeze(1).to_broadcast([P, NTILES, 4]),
+                op=ALU.mult,
+            )
+            nc.scalar.activation(out=pad_y_col[:], in_=b_col[:], func=ACT.Gelu)
+
+        stretch = const.tile([P, 1], F32)
+        between = const.tile([P, 1], F32)
+        scale_var = const.tile([P, 1], F32)
+        pad_y_some = const.tile([P, OUT], F32)
+
+        def count_valid_rows():
+            n_ps = flip_psum.tile([P, 32], F32, tag="planes")
+            nc.tensor.matmul(
+                out=n_ps[:], lhsT=spread[:].rearrange("p i q -> p (i q)"), rhs=ones[:], start=True, stop=True
+            )
+            pad_y_ps = flip_psum.tile([P, OUT], F32, tag="planes")
+            for c in range(CHUNKS):
+                nc.tensor.transpose(
+                    pad_y_ps[:, c * P : (c + 1) * P], pad_y_col[:, c : c + 1].to_broadcast([P, P]), ident[:]
+                )
+            n = const.tile([P, 1], F32)
+            nc.vector.tensor_copy(out=n[:], in_=n_ps[:, 0:1])
+            inv_n = const.tile([P, 1], F32)
+            nc.vector.tensor_scalar_max(out=inv_n[:], in0=n[:], scalar1=1.0)
+            nc.vector.reciprocal(out=inv_n[:], in_=inv_n[:])
+            some = const.tile([P, 1], F32)
+            nc.vector.tensor_scalar_min(out=some[:], in0=n[:], scalar1=1.0)
+            nc.vector.tensor_scalar(
+                out=stretch[:], in0=inv_n[:], scalar1=float(TOKENS), scalar2=some[:, 0:1], op0=ALU.mult, op1=ALU.mult
+            )
+            nc.vector.tensor_scalar(
+                out=between[:], in0=n[:], scalar1=-float(TOKENS), scalar2=float(TOKENS), op0=ALU.add, op1=ALU.mult
+            )
+            nc.vector.tensor_mul(out=between[:], in0=between[:], in1=inv_n[:])
+            inv_dof = const.tile([P, 1], F32)
+            nc.vector.tensor_scalar(out=inv_dof[:], in0=n[:], scalar1=-1.0, scalar2=1.0, op0=ALU.add, op1=ALU.max)
+            nc.vector.reciprocal(out=inv_dof[:], in_=inv_dof[:])
+            nc.vector.tensor_scalar(
+                out=scale_var[:], in0=n[:], scalar1=1.0, scalar2=inv_dof[:, 0:1], op0=ALU.is_gt, op1=ALU.mult
+            )
+            nc.vector.tensor_scalar_mul(out=pad_y_some[:], in0=pad_y_ps[:], scalar1=some[:, 0:1])
+
+        turned = {}
+
+        def turn_chunk(c):
+            d_m32 = work.tile([P, 2, SAMPLES], F32, name="d_m32", bufs=CHUNKS)
+            nc.vector.tensor_scalar(
+                out=d_m32[:, 0, :], in0=stats[:, c, :, 1], scalar1=pad_y_col[:, c : c + 1], scalar2=None, op0=ALU.subtract
+            )
+            nc.vector.tensor_copy(out=d_m32[:, 1, :], in_=stats[:, c, :, 2])
+            d_m32_t = acc_psum.tile([P, 2, P], F32, tag="acc")
+            for v in range(2):
+                nc.tensor.transpose(d_m32_t[:, v, :], d_m32[:, v, :], ident[:])
+            turned[c] = d_m32_t
+
+        result = const.tile([P, 2 * OUT], F32)
+
+        squares = {}
+
+        def square_chunk(c):
+            square = work.tile([P, P], F32, name="square", bufs=CHUNKS)
+            nc.scalar.activation(out=square[:], in_=turned[c][:, 0, :], func=ACT.Square)
+            squares[c] = square
+
+        def finish_chunk(c):
+            d_m32_t = turned[c]
+            cols = slice(c * P, (c + 1) * P)
+            within = work.tile([P, P], F32, name="within", bufs=CHUNKS)
+            nc.vector.scalar_tensor_tensor(
+                out=within[:], in0=squares[c][:], scalar=between[:, 0:1], in1=d_m32_t[:, 1, :], op0=ALU.mult, op1=ALU.add
+            )
+            nc.vector.tensor_scalar_max(out=within[:], in0=within[:], scalar1=0.0)
+            nc.vector.scalar_tensor_tensor(
+                out=result[:, OUT + c * P : OUT + (c + 1) * P],
+                in0=d_m32_t[:, 0, :],
+                scalar=stretch[:, 0:1],
+                in1=pad_y_some[:, cols],
+                op0=ALU.mult,
+                op1=ALU.add,
+            )
+            nc.scalar.activation(out=result[:, cols], in_=within[:], func=ACT.Sqrt, scale=scale_var[:, 0:1])
 
         test_rows(0)
-        make_masks(0)
-        test_rows(1)
-        make_masks(1)
         flip(0)
-        for blk in range(NBLOCKS):
-            if blk + 1 < NBLOCKS:
-                flip(blk + 1)
-            if blk + 2 < NBLOCKS:
-                test_rows(blk + 2)
-                make_masks(blk + 2)
-            layer(blk)
-
-        valid = const.tile([P, NBLOCKS * TILES], F32)
-        nc.vector.tensor_single_scalar(out=valid[:], in_=distance[:], scalar=0.0, op=ALU.is_gt)
-        spread = const.tile([P, NBLOCKS * TILES, 4], BF16)
-        nc.vector.tensor_tensor(
-            out=spread[:],
-            in0=valid[:].unsqueeze(2).to_broadcast([P, NBLOCKS * TILES, 4]),
-            in1=quadrant[:].unsqueeze(1).to_broadcast([P, NBLOCKS * TILES, 4]),
-            op=ALU.mult,
-        )
-        n_ps = flip_psum.tile([P, 32], F32, tag="planes")
-        nc.tensor.matmul(out=n_ps[:], lhsT=spread[:].rearrange("p i q -> p (i q)"), rhs=ones[:], start=True, stop=True)
-        n = const.tile([P, 1], F32)
-        nc.vector.tensor_copy(out=n[:], in_=n_ps[:, 0:1])
-        inv_n = const.tile([P, 1], F32)
-        nc.vector.tensor_scalar_max(out=inv_n[:], in0=n[:], scalar1=1.0)
-        nc.vector.reciprocal(out=inv_n[:], in_=inv_n[:])
-        some = const.tile([P, 1], F32)
-        nc.vector.tensor_scalar_min(out=some[:], in0=n[:], scalar1=1.0)
-        stretch = const.tile([P, 1], F32)
-        nc.vector.tensor_scalar(
-            out=stretch[:], in0=inv_n[:], scalar1=float(TOKENS), scalar2=some[:, 0:1], op0=ALU.mult, op1=ALU.mult
-        )
-        between = const.tile([P, 1], F32)
-        nc.vector.tensor_scalar(
-            out=between[:], in0=n[:], scalar1=-float(TOKENS), scalar2=float(TOKENS), op0=ALU.add, op1=ALU.mult
-        )
-        nc.vector.tensor_mul(out=between[:], in0=between[:], in1=inv_n[:])
-        inv_dof = const.tile([P, 1], F32)
-        nc.vector.tensor_scalar(out=inv_dof[:], in0=n[:], scalar1=-1.0, scalar2=1.0, op0=ALU.add, op1=ALU.max)
-        nc.vector.reciprocal(out=inv_dof[:], in_=inv_dof[:])
-        scale_var = const.tile([P, 1], F32)
-        nc.vector.tensor_scalar(
-            out=scale_var[:], in0=n[:], scalar1=1.0, scalar2=inv_dof[:, 0:1], op0=ALU.is_gt, op1=ALU.mult
-        )
-        pad_y_some = const.tile([P, OUT], F32)
-        nc.vector.tensor_scalar_mul(out=pad_y_some[:], in0=pad_y_rows[:], scalar1=some[:, 0:1])
-
-        shift = const.tile([P, CHUNKS, SAMPLES], F32)
-        m32 = const.tile([P, CHUNKS, SAMPLES], F32)
-        shift_t = acc_psum.tile([P, OUT], F32, tag="acc")
-        m32_t = acc_psum.tile([P, OUT], F32, tag="acc")
+        test_rows(1)
+        for blk in range(NBLOCKS - 2):
+            test_rows(blk + 2)
+            flip(blk + 1)
+            layer(blk, nothing)
+        mark_valid_rows()
+        flip(NBLOCKS - 1)
+        layer(NBLOCKS - 2, nothing)
+        count_valid_rows()
+        layer(NBLOCKS - 1, turn_chunk)
+        nc.scalar.activation(out=warm[:], in_=one[:], func=ACT.Sqrt)
         for c in range(CHUNKS):
-            nc.vector.tensor_scalar(
-                out=shift[:, c, :], in0=stats[:, c, :, 1], scalar1=pad_y_col[:, c : c + 1], scalar2=None, op0=ALU.subtract
-            )
-            nc.tensor.transpose(shift_t[:, c * P : (c + 1) * P], shift[:, c, :], ident[:])
+            square_chunk(c)
         for c in range(CHUNKS):
-            nc.vector.tensor_copy(out=m32[:, c, :], in_=stats[:, c, :, 2])
-            nc.tensor.transpose(m32_t[:, c * P : (c + 1) * P], m32[:, c, :], ident[:])
-        result = const.tile([P, 2 * OUT], F32)
-        square = const.tile([P, OUT], F32)
-        nc.scalar.activation(out=square[:], in_=shift_t[:], func=ACT.Square)
-        nc.vector.scalar_tensor_tensor(
-            out=result[:, OUT : 2 * OUT], in0=shift_t[:], scalar=stretch[:, 0:1], in1=pad_y_some[:], op0=ALU.mult, op1=ALU.add
-        )
+            finish_chunk(c)
         nc.sync.dma_start(out=out[:, OUT : 2 * OUT], in_=result[:, OUT : 2 * OUT])
-        within = const.tile([P, OUT], F32)
-        nc.vector.scalar_tensor_tensor(
-            out=within[:], in0=square[:], scalar=between[:, 0:1], in1=m32_t[:], op0=ALU.mult, op1=ALU.add
-        )
-        nc.vector.tensor_scalar_max(out=within[:], in0=within[:], scalar1=0.0)
-        nc.scalar.activation(out=result[:, 0:OUT], in_=within[:], func=ACT.Sqrt, scale=scale_var[:, 0:1])
         nc.sync.dma_start(out=out[:, 0:OUT], in_=result[:, 0:OUT])

@@ -41,7 +41,6 @@ def tile_linearnnencoder_kernel(tc, x, W_words, W_scales, b, out):
         y_pool = ctx.enter_context(tc.tile_pool(name="y_pool", bufs=6))
         flip_psum = ctx.enter_context(tc.psum_pool(name="flip_psum", bufs=4))
         acc_psum = ctx.enter_context(tc.psum_pool(name="acc_psum", bufs=4))
-        ctx.enter_context(tc.manual_schedule())
 
         x_blocks = []
         for blk in range(NBLOCKS):
@@ -134,10 +133,12 @@ def tile_linearnnencoder_kernel(tc, x, W_words, W_scales, b, out):
                             x_words[:, i, u:WORDS:2],
                             row_masks[blk][:, i, :],
                         )
-                nc.scalar.copy(
-                    out=grouped_words[:, half * BLOCK : (half + 1) * BLOCK].rearrange("p (r u) -> p r u", u=2),
-                    in_=planes[:].rearrange("p u r -> p r u"),
-                )
+                dst = grouped_words[:, half * BLOCK : (half + 1) * BLOCK].rearrange("p (r u) -> p r u", u=2)
+                src = planes[:].rearrange("p u r -> p r u")
+                if half == 0:
+                    nc.scalar.copy(out=dst, in_=src)
+                else:
+                    nc.vector.tensor_copy(out=dst, in_=src)
             x_codes = work.tile([P, BLOCK], U32, name="x_codes", align_bytes=64)
             x_scales = work.tile([P, BLOCK], U8, name="x_scales", align_bytes=64)
             nc.vector.quantize_mx(out=x_codes[:].bitcast(FP8X4), scales=x_scales[:], in_=grouped[:])
@@ -168,6 +169,7 @@ def tile_linearnnencoder_kernel(tc, x, W_words, W_scales, b, out):
                         in_=y[:, 2 * pair * TOKENS : 2 * (pair + 1) * TOKENS].rearrange("p (s t) -> p t s", s=2),
                     )
                 after_chunk(c)
+            return y
 
         def nothing(c):
             return None
@@ -274,8 +276,8 @@ def tile_linearnnencoder_kernel(tc, x, W_words, W_scales, b, out):
         flip(NBLOCKS - 1)
         layer(NBLOCKS - 2, nothing)
         count_valid_rows()
-        layer(NBLOCKS - 1, turn_chunk)
-        nc.scalar.activation(out=warm[:], in_=one[:], func=ACT.Sqrt)
+        last_y = layer(NBLOCKS - 1, turn_chunk)
+        nc.scalar.activation(out=warm[:], in_=last_y[:, 0:1], func=ACT.Sqrt, scale=0.0, bias=one[:, 0:1])
         for c in range(CHUNKS):
             square_chunk(c)
         for c in range(CHUNKS):

@@ -25,7 +25,7 @@ NBLOCKS = SAMPLES * TOKENS // BLOCK
 NTILES = NBLOCKS * TILES
 BLOCK_SAMPLES = BLOCK // TOKENS
 WORDS = K // 2
-MINUS_PAD_WORD = 1.0 + 0xBF80 / 2.0**23
+PAD_WORD = -(1.0 + 0xBF80 / 2.0**23)
 
 FLOPS = 2 * SAMPLES * TOKENS * K * OUT
 
@@ -73,8 +73,6 @@ def tile_linearnnencoder_kernel(tc, x, W_words, W_scales, b, out):
         nc.vector.memset(one[:], 1.0)
         warm = const.tile([P, 1], F32)
         nc.scalar.activation(out=warm[:], in_=one[:], func=ACT.Gelu)
-        minus_pad_word = const.tile([P, 1], F32)
-        nc.vector.memset(minus_pad_word[:], MINUS_PAD_WORD)
         ones = const.tile([P, 32], BF16)
         nc.vector.memset(ones[:], 1.0)
         quadrant = const.tile([P, 4], F32)
@@ -89,34 +87,31 @@ def tile_linearnnencoder_kernel(tc, x, W_words, W_scales, b, out):
         b_col = const.tile([P, CHUNKS], F32)
         nc.vector.tensor_copy(out=b_col[:], in_=b_ps[:, 0:CHUNKS])
 
-        distance = const.tile([P, NTILES], F32)
-        junk = const.tile([P, WORDS], F32)
+        any_differs = const.tile([P, NTILES], F32)
+        valid = const.tile([P, NTILES], F32)
         stats = const.tile([P, CHUNKS, SAMPLES, 3], F32)
 
         row_masks = {}
         codes = {}
 
-        def test_rows(blk):
-            for i in range(TILES):
-                t = blk * TILES + i
-                nc.scalar.activation(
-                    out=junk[:],
-                    in_=x_blocks[blk][:, i, :].bitcast(F32),
-                    func=ACT.Square,
-                    bias=minus_pad_word[:, 0:1],
-                    accum_out=distance[:, t : t + 1],
-                )
+        def test_rows(blk, pieces):
+            x_words = x_blocks[blk][:].bitcast(F32)
+            differs = work.tile([P, TILES, WORDS], BF16, name="differs")
             mask = work.tile([P, TILES, P], F32, name="mask")
-            for i in range(TILES):
-                t = blk * TILES + i
-                nc.vector.tensor_scalar(
-                    out=mask[:, i, :],
-                    in0=ident[:],
-                    scalar1=distance[:, t : t + 1],
-                    scalar2=0.0,
-                    op0=ALU.mult,
-                    op1=ALU.is_gt,
+            step = TILES // pieces
+            for first in range(0, TILES, step):
+                here = slice(first, first + step)
+                rows = slice(blk * TILES + first, blk * TILES + first + step)
+                nc.vector.tensor_single_scalar(
+                    out=differs[:, here, :], in_=x_words[:, here, :], scalar=PAD_WORD, op=ALU.not_equal
                 )
+                nc.vector.tensor_reduce(
+                    out=any_differs[:, rows], in_=differs[:, here, :].bitcast(I32), axis=mybir.AxisListType.X, op=ALU.max
+                )
+                nc.vector.tensor_single_scalar(out=valid[:, rows], in_=any_differs[:, rows], scalar=0.0, op=ALU.is_gt)
+                for i in range(first, first + step):
+                    t = blk * TILES + i
+                    nc.scalar.activation(out=mask[:, i, :], in_=ident[:], func=ACT.Copy, scale=valid[:, t : t + 1])
             row_masks[blk] = mask
 
         def flip(blk):
@@ -135,10 +130,7 @@ def tile_linearnnencoder_kernel(tc, x, W_words, W_scales, b, out):
                         )
                 dst = grouped_words[:, half * BLOCK : (half + 1) * BLOCK].rearrange("p (r u) -> p r u", u=2)
                 src = planes[:].rearrange("p u r -> p r u")
-                if half == 0:
-                    nc.scalar.copy(out=dst, in_=src)
-                else:
-                    nc.vector.tensor_copy(out=dst, in_=src)
+                nc.scalar.copy(out=dst, in_=src)
             x_codes = work.tile([P, BLOCK], U32, name="x_codes", align_bytes=64)
             x_scales = work.tile([P, BLOCK], U8, name="x_scales", align_bytes=64)
             nc.vector.quantize_mx(out=x_codes[:].bitcast(FP8X4), scales=x_scales[:], in_=grouped[:])
@@ -178,8 +170,6 @@ def tile_linearnnencoder_kernel(tc, x, W_words, W_scales, b, out):
         pad_y_col = const.tile([P, CHUNKS], F32)
 
         def mark_valid_rows():
-            valid = const.tile([P, NTILES], F32)
-            nc.vector.tensor_single_scalar(out=valid[:], in_=distance[:], scalar=0.0, op=ALU.is_gt)
             nc.vector.tensor_tensor(
                 out=spread[:],
                 in0=valid[:].unsqueeze(2).to_broadcast([P, NTILES, 4]),
@@ -265,11 +255,11 @@ def tile_linearnnencoder_kernel(tc, x, W_words, W_scales, b, out):
             )
             nc.scalar.activation(out=result[:, cols], in_=within[:], func=ACT.Sqrt, scale=scale_var[:, 0:1])
 
-        test_rows(0)
+        test_rows(0, TILES)
         flip(0)
-        test_rows(1)
+        test_rows(1, 1)
         for blk in range(NBLOCKS - 2):
-            test_rows(blk + 2)
+            test_rows(blk + 2, 1)
             flip(blk + 1)
             layer(blk, nothing)
         mark_valid_rows()

@@ -24,8 +24,13 @@ TILES = BLOCK // P
 NBLOCKS = SAMPLES * TOKENS // BLOCK
 NTILES = NBLOCKS * TILES
 BLOCK_SAMPLES = BLOCK // TOKENS
+QUAD = 32
+QUADRANTS = P // QUAD
+assert TOKENS == QUAD
+QUAD_SCALES = QUAD // 8
 WORDS = K // 2
 PAD_WORD = -(1.0 + 0xBF80 / 2.0**23)
+NARROW = 32
 
 FLOPS = 2 * SAMPLES * TOKENS * K * OUT
 
@@ -38,14 +43,10 @@ def tile_linearnnencoder_kernel(tc, x, W_words, W_scales, b, out):
         const = ctx.enter_context(tc.tile_pool(name="const", bufs=1))
         x_pool = ctx.enter_context(tc.tile_pool(name="x_pool", bufs=NBLOCKS))
         work = ctx.enter_context(tc.tile_pool(name="work", bufs=3))
-        y_pool = ctx.enter_context(tc.tile_pool(name="y_pool", bufs=6))
+        y_pool = ctx.enter_context(tc.tile_pool(name="y_pool", bufs=CHUNKS + 2))
+        ends = ctx.enter_context(tc.tile_pool(name="ends", bufs=CHUNKS))
         flip_psum = ctx.enter_context(tc.psum_pool(name="flip_psum", bufs=4))
-        acc_psum = ctx.enter_context(tc.psum_pool(name="acc_psum", bufs=4))
-
-        x_blocks = []
-        for blk in range(NBLOCKS):
-            x_blk = x_pool.tile([P, TILES, K], BF16, name="x_blk")
-            x_blocks.append(x_blk)
+        acc_psum = ctx.enter_context(tc.psum_pool(name="acc_psum", bufs=CHUNKS))
 
         w_words = const.tile([P, 2 * OUT], U8, align_bytes=64)
         w_scales = const.tile([P, OUT], U8, align_bytes=64)
@@ -53,19 +54,25 @@ def tile_linearnnencoder_kernel(tc, x, W_words, W_scales, b, out):
         nc.vector.memset(w_scales[:].bitcast(I32), 0)
         nc.vector.memset(b_top[:], 0.0)
         nc.scalar.dma_start(out=b_top[0:CHUNKS, :], in_=b.rearrange("(c f) -> c f", f=P))
-        for i in range(TILES):
-            nc.sync.dma_start(out=x_blocks[0][:, i, :], in_=x_rows[i * P : (i + 1) * P, :])
-        nc.sync.dma_start(out=w_words[:].bitcast(I32), in_=W_words[0].bitcast(I32))
-        for quad in range(4):
+
+        x_blocks = []
+
+        def load_block(blk):
+            x_blk = x_pool.tile([P, TILES, K], BF16, name="x_blk")
             nc.sync.dma_start(
-                out=w_scales[32 * quad : 32 * quad + 4, :].bitcast(I32),
-                in_=W_scales[0, 4 * quad : 4 * quad + 4, :].bitcast(I32),
+                out=x_blk[:], in_=x_rows[blk * BLOCK : (blk + 1) * BLOCK, :].rearrange("(i p) k -> p i k", p=P)
+            )
+            x_blocks.append(x_blk)
+
+        load_block(0)
+        nc.sync.dma_start(out=w_words[:].bitcast(I32), in_=W_words[0].bitcast(I32))
+        for q in range(QUADRANTS):
+            nc.sync.dma_start(
+                out=w_scales[QUAD * q : QUAD * q + QUAD_SCALES, :].bitcast(I32),
+                in_=W_scales[0, QUAD_SCALES * q : QUAD_SCALES * (q + 1), :].bitcast(I32),
             )
         for blk in range(1, NBLOCKS):
-            nc.sync.dma_start(
-                out=x_blocks[blk][:],
-                in_=x_rows[blk * BLOCK : (blk + 1) * BLOCK, :].rearrange("(i p) k -> p i k", p=P),
-            )
+            load_block(blk)
 
         ident = const.tile([P, P], F32)
         make_identity(nc, ident[:])
@@ -73,16 +80,16 @@ def tile_linearnnencoder_kernel(tc, x, W_words, W_scales, b, out):
         nc.vector.memset(one[:], 1.0)
         warm = const.tile([P, 1], F32)
         nc.scalar.activation(out=warm[:], in_=one[:], func=ACT.Gelu)
-        ones = const.tile([P, 32], BF16)
+        ones = const.tile([P, NARROW], BF16)
         nc.vector.memset(ones[:], 1.0)
-        quadrant = const.tile([P, 4], F32)
+        quadrant = const.tile([P, QUADRANTS], F32)
         nc.vector.memset(quadrant[:], 0.0)
-        for quad in range(4):
-            nc.vector.memset(quadrant[32 * quad : 32 * quad + 32, quad : quad + 1], 1.0)
-        ident_bf = const.tile([P, 32], BF16)
-        nc.vector.tensor_copy(out=ident_bf[:], in_=ident[:, 0:32])
+        for q in range(QUADRANTS):
+            nc.vector.memset(quadrant[QUAD * q : QUAD * (q + 1), q : q + 1], 1.0)
+        ident_bf = const.tile([P, NARROW], BF16)
+        nc.vector.tensor_copy(out=ident_bf[:], in_=ident[:, 0:NARROW])
 
-        b_ps = acc_psum.tile([P, 32], F32, tag="acc")
+        b_ps = acc_psum.tile([P, NARROW], F32, tag="acc")
         nc.tensor.matmul(out=b_ps[:], lhsT=b_top[:], rhs=ident_bf[:], start=True, stop=True)
         b_col = const.tile([P, CHUNKS], F32)
         nc.vector.tensor_copy(out=b_col[:], in_=b_ps[:, 0:CHUNKS])
@@ -92,26 +99,23 @@ def tile_linearnnencoder_kernel(tc, x, W_words, W_scales, b, out):
         stats = const.tile([P, CHUNKS, SAMPLES, 3], F32)
 
         row_masks = {}
-        codes = {}
+        quantised = {}
+        sums = {}
 
-        def test_rows(blk, pieces):
-            x_words = x_blocks[blk][:].bitcast(F32)
+        def test_rows(blk):
+            tiles = slice(blk * TILES, (blk + 1) * TILES)
             differs = work.tile([P, TILES, WORDS], BF16, name="differs")
+            nc.vector.tensor_single_scalar(
+                out=differs[:], in_=x_blocks[blk][:].bitcast(F32), scalar=PAD_WORD, op=ALU.not_equal
+            )
+            nc.vector.tensor_reduce(
+                out=any_differs[:, tiles], in_=differs[:].bitcast(I32), axis=mybir.AxisListType.X, op=ALU.max
+            )
+            nc.vector.tensor_single_scalar(out=valid[:, tiles], in_=any_differs[:, tiles], scalar=0.0, op=ALU.is_gt)
             mask = work.tile([P, TILES, P], F32, name="mask")
-            step = TILES // pieces
-            for first in range(0, TILES, step):
-                here = slice(first, first + step)
-                rows = slice(blk * TILES + first, blk * TILES + first + step)
-                nc.vector.tensor_single_scalar(
-                    out=differs[:, here, :], in_=x_words[:, here, :], scalar=PAD_WORD, op=ALU.not_equal
-                )
-                nc.vector.tensor_reduce(
-                    out=any_differs[:, rows], in_=differs[:, here, :].bitcast(I32), axis=mybir.AxisListType.X, op=ALU.max
-                )
-                nc.vector.tensor_single_scalar(out=valid[:, rows], in_=any_differs[:, rows], scalar=0.0, op=ALU.is_gt)
-                for i in range(first, first + step):
-                    t = blk * TILES + i
-                    nc.scalar.activation(out=mask[:, i, :], in_=ident[:], func=ACT.Copy, scale=valid[:, t : t + 1])
+            for i in range(TILES):
+                t = blk * TILES + i
+                nc.scalar.activation(out=mask[:, i, :], in_=ident[:], func=ACT.Copy, scale=valid[:, t : t + 1])
             row_masks[blk] = mask
 
         def flip(blk):
@@ -124,21 +128,19 @@ def tile_linearnnencoder_kernel(tc, x, W_words, W_scales, b, out):
                     i = 2 * half + j
                     for u in range(2):
                         nc.tensor.transpose(
-                            planes[:, u, j * P : (j + 1) * P],
-                            x_words[:, i, u:WORDS:2],
-                            row_masks[blk][:, i, :],
+                            planes[:, u, j * P : (j + 1) * P], x_words[:, i, u:WORDS:2], row_masks[blk][:, i, :]
                         )
-                dst = grouped_words[:, half * BLOCK : (half + 1) * BLOCK].rearrange("p (r u) -> p r u", u=2)
-                src = planes[:].rearrange("p u r -> p r u")
-                nc.scalar.copy(out=dst, in_=src)
+                nc.scalar.copy(
+                    out=grouped_words[:, half * BLOCK : (half + 1) * BLOCK].rearrange("p (r u) -> p r u", u=2),
+                    in_=planes[:].rearrange("p u r -> p r u"),
+                )
             x_codes = work.tile([P, BLOCK], U32, name="x_codes", align_bytes=64)
             x_scales = work.tile([P, BLOCK], U8, name="x_scales", align_bytes=64)
             nc.vector.quantize_mx(out=x_codes[:].bitcast(FP8X4), scales=x_scales[:], in_=grouped[:])
-            codes[blk] = (x_codes, x_scales)
+            quantised[blk] = (x_codes, x_scales)
 
-        def layer(blk, after_chunk):
-            x_codes, x_scales = codes[blk]
-            accs = []
+        def multiply(blk):
+            x_codes, x_scales = quantised[blk]
             for c in range(CHUNKS):
                 acc = acc_psum.tile([P, BLOCK], F32, name="acc")
                 nc.tensor.matmul_mx(
@@ -150,30 +152,27 @@ def tile_linearnnencoder_kernel(tc, x, W_words, W_scales, b, out):
                     start=True,
                     stop=True,
                 )
-                accs.append(acc)
-            for c in range(CHUNKS):
-                y = y_pool.tile([P, BLOCK], F32, name="y")
-                nc.scalar.activation(out=y[:], in_=accs[c][:], func=ACT.Gelu, bias=b_col[:, c : c + 1])
-                for pair in range(BLOCK_SAMPLES // 2):
-                    s = blk * BLOCK_SAMPLES + 2 * pair
-                    nc.vector.bn_stats(
-                        out=stats[:, c, s : s + 2, :].rearrange("p s v -> p (s v)"),
-                        in_=y[:, 2 * pair * TOKENS : 2 * (pair + 1) * TOKENS].rearrange("p (s t) -> p t s", s=2),
-                    )
-                after_chunk(c)
+                sums[c] = acc
+
+        def activate(blk, c):
+            y = y_pool.tile([P, BLOCK], F32, name="y")
+            nc.scalar.activation(out=y[:], in_=sums[c][:], func=ACT.Gelu, bias=b_col[:, c : c + 1])
+            for pair in range(BLOCK_SAMPLES // 2):
+                s = blk * BLOCK_SAMPLES + 2 * pair
+                nc.vector.bn_stats(
+                    out=stats[:, c, s : s + 2, :].rearrange("p s v -> p (s v)"),
+                    in_=y[:, 2 * pair * TOKENS : 2 * (pair + 1) * TOKENS].rearrange("p (s t) -> p t s", s=2),
+                )
             return y
 
-        def nothing(c):
-            return None
-
-        spread = const.tile([P, NTILES, 4], BF16)
+        spread = const.tile([P, NTILES, QUADRANTS], BF16)
         pad_y_col = const.tile([P, CHUNKS], F32)
 
         def mark_valid_rows():
             nc.vector.tensor_tensor(
                 out=spread[:],
-                in0=valid[:].unsqueeze(2).to_broadcast([P, NTILES, 4]),
-                in1=quadrant[:].unsqueeze(1).to_broadcast([P, NTILES, 4]),
+                in0=valid[:].unsqueeze(2).to_broadcast([P, NTILES, QUADRANTS]),
+                in1=quadrant[:].unsqueeze(1).to_broadcast([P, NTILES, QUADRANTS]),
                 op=ALU.mult,
             )
             nc.scalar.activation(out=pad_y_col[:], in_=b_col[:], func=ACT.Gelu)
@@ -184,7 +183,7 @@ def tile_linearnnencoder_kernel(tc, x, W_words, W_scales, b, out):
         pad_y_some = const.tile([P, OUT], F32)
 
         def count_valid_rows():
-            n_ps = flip_psum.tile([P, 32], F32, tag="planes")
+            n_ps = flip_psum.tile([P, NARROW], F32, tag="planes")
             nc.tensor.matmul(
                 out=n_ps[:], lhsT=spread[:].rearrange("p i q -> p (i q)"), rhs=ones[:], start=True, stop=True
             )
@@ -216,9 +215,11 @@ def tile_linearnnencoder_kernel(tc, x, W_words, W_scales, b, out):
             nc.vector.tensor_scalar_mul(out=pad_y_some[:], in0=pad_y_ps[:], scalar1=some[:, 0:1])
 
         turned = {}
+        squares = {}
+        result = const.tile([P, 2 * OUT], F32)
 
         def turn_chunk(c):
-            d_m32 = work.tile([P, 2, SAMPLES], F32, name="d_m32", bufs=CHUNKS)
+            d_m32 = ends.tile([P, 2, SAMPLES], F32, name="d_m32")
             nc.vector.tensor_scalar(
                 out=d_m32[:, 0, :], in0=stats[:, c, :, 1], scalar1=pad_y_col[:, c : c + 1], scalar2=None, op0=ALU.subtract
             )
@@ -228,19 +229,15 @@ def tile_linearnnencoder_kernel(tc, x, W_words, W_scales, b, out):
                 nc.tensor.transpose(d_m32_t[:, v, :], d_m32[:, v, :], ident[:])
             turned[c] = d_m32_t
 
-        result = const.tile([P, 2 * OUT], F32)
-
-        squares = {}
-
         def square_chunk(c):
-            square = work.tile([P, P], F32, name="square", bufs=CHUNKS)
+            square = ends.tile([P, P], F32, name="square")
             nc.scalar.activation(out=square[:], in_=turned[c][:, 0, :], func=ACT.Square)
             squares[c] = square
 
         def finish_chunk(c):
             d_m32_t = turned[c]
             cols = slice(c * P, (c + 1) * P)
-            within = work.tile([P, P], F32, name="within", bufs=CHUNKS)
+            within = ends.tile([P, P], F32, name="within")
             nc.vector.scalar_tensor_tensor(
                 out=within[:], in0=squares[c][:], scalar=between[:, 0:1], in1=d_m32_t[:, 1, :], op0=ALU.mult, op1=ALU.add
             )
@@ -255,18 +252,25 @@ def tile_linearnnencoder_kernel(tc, x, W_words, W_scales, b, out):
             )
             nc.scalar.activation(out=result[:, cols], in_=within[:], func=ACT.Sqrt, scale=scale_var[:, 0:1])
 
-        test_rows(0, TILES)
+        test_rows(0)
         flip(0)
-        test_rows(1, 1)
+        test_rows(1)
         for blk in range(NBLOCKS - 2):
-            test_rows(blk + 2, 1)
+            test_rows(blk + 2)
             flip(blk + 1)
-            layer(blk, nothing)
+            multiply(blk)
+            for c in range(CHUNKS):
+                activate(blk, c)
         mark_valid_rows()
         flip(NBLOCKS - 1)
-        layer(NBLOCKS - 2, nothing)
+        multiply(NBLOCKS - 2)
+        for c in range(CHUNKS):
+            activate(NBLOCKS - 2, c)
         count_valid_rows()
-        last_y = layer(NBLOCKS - 1, turn_chunk)
+        multiply(NBLOCKS - 1)
+        for c in range(CHUNKS):
+            last_y = activate(NBLOCKS - 1, c)
+            turn_chunk(c)
         nc.scalar.activation(out=warm[:], in_=last_y[:, 0:1], func=ACT.Sqrt, scale=0.0, bias=one[:, 0:1])
         for c in range(CHUNKS):
             square_chunk(c)

@@ -30,6 +30,13 @@ assert TOKENS == QUAD
 QUAD_SCALES = QUAD // 8
 WORDS = K // 2
 PAD_WORD = -(1.0 + 0xBF80 / 2.0**23)
+UNIT_TILES = (4, 4, 4, 4, 4, 4, 4, 4)
+NUNITS = len(UNIT_TILES)
+UNIT_START = tuple(sum(UNIT_TILES[:u]) for u in range(NUNITS))
+assert sum(UNIT_TILES) == NTILES and max(UNIT_TILES) == TILES
+TILE_SAMPLES = P // TOKENS
+SCALAR_TESTS = 1
+AHEAD = 4
 NARROW = 32
 
 FLOPS = 2 * SAMPLES * TOKENS * K * OUT
@@ -41,8 +48,9 @@ def tile_linearnnencoder_kernel(tc, x, W_words, W_scales, b, out):
 
     with ExitStack() as ctx:
         const = ctx.enter_context(tc.tile_pool(name="const", bufs=1))
-        x_pool = ctx.enter_context(tc.tile_pool(name="x_pool", bufs=NBLOCKS))
+        x_pool = ctx.enter_context(tc.tile_pool(name="x_pool", bufs=NUNITS))
         work = ctx.enter_context(tc.tile_pool(name="work", bufs=3))
+        mask_pool = ctx.enter_context(tc.tile_pool(name="mask_pool", bufs=AHEAD + 1))
         y_pool = ctx.enter_context(tc.tile_pool(name="y_pool", bufs=CHUNKS + 2))
         ends = ctx.enter_context(tc.tile_pool(name="ends", bufs=CHUNKS))
         flip_psum = ctx.enter_context(tc.psum_pool(name="flip_psum", bufs=4))
@@ -51,33 +59,36 @@ def tile_linearnnencoder_kernel(tc, x, W_words, W_scales, b, out):
         w_words = const.tile([P, 2 * OUT], U8, align_bytes=64)
         w_scales = const.tile([P, OUT], U8, align_bytes=64)
         b_top = const.tile([P, P], BF16)
-        nc.vector.memset(w_scales[:].bitcast(I32), 0)
         nc.vector.memset(b_top[:], 0.0)
-        nc.scalar.dma_start(out=b_top[0:CHUNKS, :], in_=b.rearrange("(c f) -> c f", f=P))
+        nc.vector.memset(w_scales[:].bitcast(I32), 0)
+        nc.sync.dma_start(out=b_top[0:CHUNKS, :], in_=b.rearrange("(c f) -> c f", f=P))
 
-        x_blocks = []
+        x_units = []
 
-        def load_block(blk):
-            x_blk = x_pool.tile([P, TILES, K], BF16, name="x_blk")
+        def load_unit(u):
+            first, n = UNIT_START[u], UNIT_TILES[u]
+            x_unit = x_pool.tile([P, n, K], BF16, name="x_unit")
             nc.sync.dma_start(
-                out=x_blk[:], in_=x_rows[blk * BLOCK : (blk + 1) * BLOCK, :].rearrange("(i p) k -> p i k", p=P)
+                out=x_unit[:], in_=x_rows[first * P : (first + n) * P, :].rearrange("(i p) k -> p i k", p=P)
             )
-            x_blocks.append(x_blk)
+            x_units.append(x_unit)
 
-        load_block(0)
+        load_unit(0)
         nc.sync.dma_start(out=w_words[:].bitcast(I32), in_=W_words[0].bitcast(I32))
         for q in range(QUADRANTS):
             nc.sync.dma_start(
                 out=w_scales[QUAD * q : QUAD * q + QUAD_SCALES, :].bitcast(I32),
                 in_=W_scales[0, QUAD_SCALES * q : QUAD_SCALES * (q + 1), :].bitcast(I32),
             )
-        for blk in range(1, NBLOCKS):
-            load_block(blk)
+        for u in range(1, NUNITS):
+            load_unit(u)
 
         ident = const.tile([P, P], F32)
         make_identity(nc, ident[:])
         one = const.tile([P, 1], F32)
         nc.vector.memset(one[:], 1.0)
+        minus_pad_word = const.tile([P, 1], F32)
+        nc.vector.memset(minus_pad_word[:], -PAD_WORD)
         warm = const.tile([P, 1], F32)
         nc.scalar.activation(out=warm[:], in_=one[:], func=ACT.Gelu)
         ones = const.tile([P, NARROW], BF16)
@@ -102,47 +113,66 @@ def tile_linearnnencoder_kernel(tc, x, W_words, W_scales, b, out):
         quantised = {}
         sums = {}
 
-        def test_rows(blk):
-            tiles = slice(blk * TILES, (blk + 1) * TILES)
-            differs = work.tile([P, TILES, WORDS], BF16, name="differs")
+        def test_rows(u):
+            first, n = UNIT_START[u], UNIT_TILES[u]
+            on_scalar = SCALAR_TESTS if n == TILES else 0
+            on_vector = n - on_scalar
+            x_words = x_units[u][:].bitcast(F32)
+            differs = work.tile([P, on_vector, WORDS], BF16, name="differs")
             nc.vector.tensor_single_scalar(
-                out=differs[:], in_=x_blocks[blk][:].bitcast(F32), scalar=PAD_WORD, op=ALU.not_equal
+                out=differs[:], in_=x_words[:, 0:on_vector, :], scalar=PAD_WORD, op=ALU.not_equal
             )
             nc.vector.tensor_reduce(
-                out=any_differs[:, tiles], in_=differs[:].bitcast(I32), axis=mybir.AxisListType.X, op=ALU.max
+                out=any_differs[:, first : first + on_vector],
+                in_=differs[:].bitcast(I32),
+                axis=mybir.AxisListType.X,
+                op=ALU.max,
             )
-            nc.vector.tensor_single_scalar(out=valid[:, tiles], in_=any_differs[:, tiles], scalar=0.0, op=ALU.is_gt)
-            mask = work.tile([P, TILES, P], F32, name="mask")
-            for i in range(TILES):
-                t = blk * TILES + i
-                nc.scalar.activation(out=mask[:, i, :], in_=ident[:], func=ACT.Copy, scale=valid[:, t : t + 1])
-            row_masks[blk] = mask
+            for i in range(on_vector, n):
+                distance = work.tile([P, WORDS], BF16, name="distance")
+                nc.scalar.activation(
+                    out=distance[:],
+                    in_=x_words[:, i, :],
+                    func=ACT.Abs,
+                    bias=minus_pad_word[:, 0:1],
+                    accum_out=any_differs[:, first + i : first + i + 1],
+                )
+            tiles = slice(first, first + n)
+            nc.gpsimd.tensor_single_scalar(out=valid[:, tiles], in_=any_differs[:, tiles], scalar=0.0, op=ALU.is_gt)
+            mask = mask_pool.tile([P, n, P], F32, name="mask")
+            for i in range(n):
+                t = first + i
+                nc.gpsimd.tensor_scalar(
+                    out=mask[:, i, :], in0=ident[:], scalar1=valid[:, t : t + 1], scalar2=0.0, op0=ALU.mult, op1=ALU.add
+                )
+            row_masks[u] = mask
 
-        def flip(blk):
-            x_words = x_blocks[blk][:].bitcast(F32)
-            grouped = work.tile([P, 4 * BLOCK], BF16, name="grouped", align_bytes=64)
+        def flip(u):
+            n = UNIT_TILES[u]
+            x_words = x_units[u][:].bitcast(F32)
+            grouped = work.tile([P, 4 * n * P], BF16, name="grouped", align_bytes=64)
             grouped_words = grouped[:].bitcast(F32)
-            for half in range(2):
-                planes = flip_psum.tile([P, 2, 2 * P], F32, name="planes")
-                for j in range(2):
-                    i = 2 * half + j
-                    for u in range(2):
+            for start in range(0, n, 2):
+                m = min(2, n - start)
+                planes = flip_psum.tile([P, 2, m * P], F32, name="planes")
+                for j in range(m):
+                    for w in range(2):
                         nc.tensor.transpose(
-                            planes[:, u, j * P : (j + 1) * P], x_words[:, i, u:WORDS:2], row_masks[blk][:, i, :]
+                            planes[:, w, j * P : (j + 1) * P], x_words[:, start + j, w:WORDS:2], row_masks[u][:, start + j, :]
                         )
                 nc.scalar.copy(
-                    out=grouped_words[:, half * BLOCK : (half + 1) * BLOCK].rearrange("p (r u) -> p r u", u=2),
-                    in_=planes[:].rearrange("p u r -> p r u"),
+                    out=grouped_words[:, 2 * start * P : 2 * (start + m) * P].rearrange("p (r w) -> p r w", w=2),
+                    in_=planes[:].rearrange("p w r -> p r w"),
                 )
-            x_codes = work.tile([P, BLOCK], U32, name="x_codes", align_bytes=64)
-            x_scales = work.tile([P, BLOCK], U8, name="x_scales", align_bytes=64)
+            x_codes = work.tile([P, n * P], U32, name="x_codes", align_bytes=64)
+            x_scales = work.tile([P, n * P], U8, name="x_scales", align_bytes=64)
             nc.vector.quantize_mx(out=x_codes[:].bitcast(FP8X4), scales=x_scales[:], in_=grouped[:])
-            quantised[blk] = (x_codes, x_scales)
+            quantised[u] = (x_codes, x_scales)
 
-        def multiply(blk):
-            x_codes, x_scales = quantised[blk]
+        def multiply(u):
+            x_codes, x_scales = quantised[u]
             for c in range(CHUNKS):
-                acc = acc_psum.tile([P, BLOCK], F32, name="acc")
+                acc = acc_psum.tile([P, UNIT_TILES[u] * P], F32, name="acc")
                 nc.tensor.matmul_mx(
                     out=acc[:],
                     lhsT=w_words[:, 2 * c * P : 2 * (c + 1) * P].bitcast(FP4X4),
@@ -154,11 +184,11 @@ def tile_linearnnencoder_kernel(tc, x, W_words, W_scales, b, out):
                 )
                 sums[c] = acc
 
-        def activate(blk, c):
-            y = y_pool.tile([P, BLOCK], F32, name="y")
+        def activate(u, c):
+            y = y_pool.tile([P, UNIT_TILES[u] * P], F32, name="y")
             nc.scalar.activation(out=y[:], in_=sums[c][:], func=ACT.Gelu, bias=b_col[:, c : c + 1])
-            for pair in range(BLOCK_SAMPLES // 2):
-                s = blk * BLOCK_SAMPLES + 2 * pair
+            for pair in range(UNIT_TILES[u] * TILE_SAMPLES // 2):
+                s = UNIT_START[u] * TILE_SAMPLES + 2 * pair
                 nc.vector.bn_stats(
                     out=stats[:, c, s : s + 2, :].rearrange("p s v -> p (s v)"),
                     in_=y[:, 2 * pair * TOKENS : 2 * (pair + 1) * TOKENS].rearrange("p (s t) -> p t s", s=2),
@@ -254,23 +284,22 @@ def tile_linearnnencoder_kernel(tc, x, W_words, W_scales, b, out):
 
         test_rows(0)
         flip(0)
-        test_rows(1)
-        for blk in range(NBLOCKS - 2):
-            test_rows(blk + 2)
-            flip(blk + 1)
-            multiply(blk)
+        for u in range(1, AHEAD):
+            test_rows(u)
+        for u in range(NUNITS):
+            if u + AHEAD < NUNITS:
+                test_rows(u + AHEAD)
+            if u + AHEAD == NUNITS:
+                mark_valid_rows()
+            if u + 1 < NUNITS:
+                flip(u + 1)
+            if u + 1 == NUNITS:
+                count_valid_rows()
+            multiply(u)
             for c in range(CHUNKS):
-                activate(blk, c)
-        mark_valid_rows()
-        flip(NBLOCKS - 1)
-        multiply(NBLOCKS - 2)
-        for c in range(CHUNKS):
-            activate(NBLOCKS - 2, c)
-        count_valid_rows()
-        multiply(NBLOCKS - 1)
-        for c in range(CHUNKS):
-            last_y = activate(NBLOCKS - 1, c)
-            turn_chunk(c)
+                last_y = activate(u, c)
+                if u + 1 == NUNITS:
+                    turn_chunk(c)
         nc.scalar.activation(out=warm[:], in_=last_y[:, 0:1], func=ACT.Sqrt, scale=0.0, bias=one[:, 0:1])
         for c in range(CHUNKS):
             square_chunk(c)

@@ -35,8 +35,8 @@ NUNITS = len(UNIT_TILES)
 UNIT_START = tuple(sum(UNIT_TILES[:u]) for u in range(NUNITS))
 assert sum(UNIT_TILES) == NTILES and max(UNIT_TILES) == TILES
 TILE_SAMPLES = P // TOKENS
-SCALAR_TESTS = 1
-AHEAD = 4
+SCALAR_TESTS = 2
+AHEAD = 3
 NARROW = 32
 
 FLOPS = 2 * SAMPLES * TOKENS * K * OUT
@@ -107,7 +107,7 @@ def tile_linearnnencoder_kernel(tc, x, W_words, W_scales, b, out):
 
         any_differs = const.tile([P, NTILES], F32)
         valid = const.tile([P, NTILES], F32)
-        stats = const.tile([P, CHUNKS, SAMPLES, 3], F32)
+        stats = const.tile([P, CHUNKS, 3, SAMPLES], F32)
 
         row_masks = {}
         quantised = {}
@@ -138,13 +138,11 @@ def tile_linearnnencoder_kernel(tc, x, W_words, W_scales, b, out):
                     accum_out=any_differs[:, first + i : first + i + 1],
                 )
             tiles = slice(first, first + n)
-            nc.gpsimd.tensor_single_scalar(out=valid[:, tiles], in_=any_differs[:, tiles], scalar=0.0, op=ALU.is_gt)
+            nc.vector.tensor_single_scalar(out=valid[:, tiles], in_=any_differs[:, tiles], scalar=0.0, op=ALU.is_gt)
             mask = mask_pool.tile([P, n, P], F32, name="mask")
             for i in range(n):
                 t = first + i
-                nc.gpsimd.tensor_scalar(
-                    out=mask[:, i, :], in0=ident[:], scalar1=valid[:, t : t + 1], scalar2=0.0, op0=ALU.mult, op1=ALU.add
-                )
+                nc.vector.tensor_scalar_mul(out=mask[:, i, :], in0=ident[:], scalar1=valid[:, t : t + 1])
             row_masks[u] = mask
 
         def flip(u):
@@ -190,7 +188,7 @@ def tile_linearnnencoder_kernel(tc, x, W_words, W_scales, b, out):
             for pair in range(UNIT_TILES[u] * TILE_SAMPLES // 2):
                 s = UNIT_START[u] * TILE_SAMPLES + 2 * pair
                 nc.vector.bn_stats(
-                    out=stats[:, c, s : s + 2, :].rearrange("p s v -> p (s v)"),
+                    out=stats[:, c, :, s : s + 2].rearrange("p v s -> p s v"),
                     in_=y[:, 2 * pair * TOKENS : 2 * (pair + 1) * TOKENS].rearrange("p (s t) -> p t s", s=2),
                 )
             return y
@@ -249,14 +247,13 @@ def tile_linearnnencoder_kernel(tc, x, W_words, W_scales, b, out):
         result = const.tile([P, 2 * OUT], F32)
 
         def turn_chunk(c):
-            d_m32 = ends.tile([P, 2, SAMPLES], F32, name="d_m32")
+            d = ends.tile([P, SAMPLES], F32, name="d")
             nc.vector.tensor_scalar(
-                out=d_m32[:, 0, :], in0=stats[:, c, :, 1], scalar1=pad_y_col[:, c : c + 1], scalar2=None, op0=ALU.subtract
+                out=d[:], in0=stats[:, c, 1, :], scalar1=pad_y_col[:, c : c + 1], scalar2=None, op0=ALU.subtract
             )
-            nc.vector.tensor_copy(out=d_m32[:, 1, :], in_=stats[:, c, :, 2])
             d_m32_t = acc_psum.tile([P, 2, P], F32, tag="acc")
-            for v in range(2):
-                nc.tensor.transpose(d_m32_t[:, v, :], d_m32[:, v, :], ident[:])
+            nc.tensor.transpose(d_m32_t[:, 0, :], d[:], ident[:])
+            nc.tensor.transpose(d_m32_t[:, 1, :], stats[:, c, 2, :], ident[:])
             turned[c] = d_m32_t
 
         def square_chunk(c):

@@ -35,7 +35,7 @@ NUNITS = len(UNIT_TILES)
 UNIT_START = tuple(sum(UNIT_TILES[:u]) for u in range(NUNITS))
 assert sum(UNIT_TILES) == NTILES and max(UNIT_TILES) == TILES
 TILE_SAMPLES = P // TOKENS
-SCALAR_TESTS = 2
+SCALAR_TESTS = 1
 AHEAD = 3
 NARROW = 32
 
@@ -74,13 +74,14 @@ def tile_linearnnencoder_kernel(tc, x, W_words, W_scales, b, out):
             x_units.append(x_unit)
 
         load_unit(0)
+        load_unit(1)
         nc.sync.dma_start(out=w_words[:].bitcast(I32), in_=W_words[0].bitcast(I32))
         for q in range(QUADRANTS):
             nc.sync.dma_start(
                 out=w_scales[QUAD * q : QUAD * q + QUAD_SCALES, :].bitcast(I32),
                 in_=W_scales[0, QUAD_SCALES * q : QUAD_SCALES * (q + 1), :].bitcast(I32),
             )
-        for u in range(1, NUNITS):
+        for u in range(2, NUNITS):
             load_unit(u)
 
         ident = const.tile([P, P], F32)
@@ -106,7 +107,6 @@ def tile_linearnnencoder_kernel(tc, x, W_words, W_scales, b, out):
         nc.vector.tensor_copy(out=b_col[:], in_=b_ps[:, 0:CHUNKS])
 
         any_differs = const.tile([P, NTILES], F32)
-        valid = const.tile([P, NTILES], F32)
         stats = const.tile([P, CHUNKS, 3, SAMPLES], F32)
 
         row_masks = {}
@@ -137,12 +137,17 @@ def tile_linearnnencoder_kernel(tc, x, W_words, W_scales, b, out):
                     bias=minus_pad_word[:, 0:1],
                     accum_out=any_differs[:, first + i : first + i + 1],
                 )
-            tiles = slice(first, first + n)
-            nc.vector.tensor_single_scalar(out=valid[:, tiles], in_=any_differs[:, tiles], scalar=0.0, op=ALU.is_gt)
             mask = mask_pool.tile([P, n, P], F32, name="mask")
             for i in range(n):
                 t = first + i
-                nc.vector.tensor_scalar_mul(out=mask[:, i, :], in0=ident[:], scalar1=valid[:, t : t + 1])
+                nc.vector.tensor_scalar(
+                    out=mask[:, i, :],
+                    in0=ident[:],
+                    scalar1=any_differs[:, t : t + 1],
+                    scalar2=0.0,
+                    op0=ALU.mult,
+                    op1=ALU.is_gt,
+                )
             row_masks[u] = mask
 
         def flip(u):
@@ -197,11 +202,13 @@ def tile_linearnnencoder_kernel(tc, x, W_words, W_scales, b, out):
         pad_y_col = const.tile([P, CHUNKS], F32)
 
         def mark_valid_rows():
-            nc.vector.tensor_tensor(
+            nc.vector.scalar_tensor_tensor(
                 out=spread[:],
-                in0=valid[:].unsqueeze(2).to_broadcast([P, NTILES, QUADRANTS]),
+                in0=any_differs[:].unsqueeze(2).to_broadcast([P, NTILES, QUADRANTS]),
+                scalar=0.0,
                 in1=quadrant[:].unsqueeze(1).to_broadcast([P, NTILES, QUADRANTS]),
-                op=ALU.mult,
+                op0=ALU.is_gt,
+                op1=ALU.mult,
             )
             nc.scalar.activation(out=pad_y_col[:], in_=b_col[:], func=ACT.Gelu)
 

@@ -35,7 +35,7 @@ NUNITS = len(UNIT_TILES)
 UNIT_START = tuple(sum(UNIT_TILES[:u]) for u in range(NUNITS))
 assert sum(UNIT_TILES) == NTILES and max(UNIT_TILES) == TILES
 TILE_SAMPLES = P // TOKENS
-SCALAR_TESTS = 1
+SCALAR_TESTS = 2
 AHEAD = 3
 NARROW = 32
 

@@ -30,13 +30,11 @@ assert TOKENS == QUAD
 QUAD_SCALES = QUAD // 8
 WORDS = K // 2
 PAD_WORD = -(1.0 + 0xBF80 / 2.0**23)
-UNIT_TILES = (4, 4, 4, 4, 4, 4, 4, 4)
-NUNITS = len(UNIT_TILES)
-UNIT_START = tuple(sum(UNIT_TILES[:u]) for u in range(NUNITS))
-assert sum(UNIT_TILES) == NTILES and max(UNIT_TILES) == TILES
 TILE_SAMPLES = P // TOKENS
-SCALAR_TESTS = 2
-AHEAD = 3
+PAIRS = BLOCK_SAMPLES // 2
+ON_VECTOR = 2
+AHEAD = 5
+EARLY = 4
 NARROW = 32
 
 FLOPS = 2 * SAMPLES * TOKENS * K * OUT
@@ -48,41 +46,42 @@ def tile_linearnnencoder_kernel(tc, x, W_words, W_scales, b, out):
 
     with ExitStack() as ctx:
         const = ctx.enter_context(tc.tile_pool(name="const", bufs=1))
-        x_pool = ctx.enter_context(tc.tile_pool(name="x_pool", bufs=NUNITS))
+        x_pool = ctx.enter_context(tc.tile_pool(name="x_pool", bufs=NBLOCKS))
         work = ctx.enter_context(tc.tile_pool(name="work", bufs=3))
         mask_pool = ctx.enter_context(tc.tile_pool(name="mask_pool", bufs=AHEAD + 1))
-        y_pool = ctx.enter_context(tc.tile_pool(name="y_pool", bufs=CHUNKS + 2))
+        y_pool = ctx.enter_context(tc.tile_pool(name="y_pool", bufs=2 * CHUNKS))
         ends = ctx.enter_context(tc.tile_pool(name="ends", bufs=CHUNKS))
         flip_psum = ctx.enter_context(tc.psum_pool(name="flip_psum", bufs=4))
         acc_psum = ctx.enter_context(tc.psum_pool(name="acc_psum", bufs=CHUNKS))
+        ctx.enter_context(tc.manual_schedule())
 
         w_words = const.tile([P, 2 * OUT], U8, align_bytes=64)
         w_scales = const.tile([P, OUT], U8, align_bytes=64)
         b_top = const.tile([P, P], BF16)
         nc.vector.memset(b_top[:], 0.0)
         nc.vector.memset(w_scales[:].bitcast(I32), 0)
-        nc.sync.dma_start(out=b_top[0:CHUNKS, :], in_=b.rearrange("(c f) -> c f", f=P))
 
-        x_units = []
+        x_blocks = []
 
-        def load_unit(u):
-            first, n = UNIT_START[u], UNIT_TILES[u]
-            x_unit = x_pool.tile([P, n, K], BF16, name="x_unit")
+        def load_block(u):
+            x_block = x_pool.tile([P, TILES, K], BF16, name="x_block")
             nc.sync.dma_start(
-                out=x_unit[:], in_=x_rows[first * P : (first + n) * P, :].rearrange("(i p) k -> p i k", p=P)
+                out=x_block[:], in_=x_rows[u * BLOCK : (u + 1) * BLOCK, :].rearrange("(i p) k -> p i k", p=P)
             )
-            x_units.append(x_unit)
+            x_blocks.append(x_block)
 
-        load_unit(0)
-        load_unit(1)
+        load_block(0)
+        nc.sync.dma_start(out=b_top[0:CHUNKS, :], in_=b.rearrange("(c f) -> c f", f=P))
+        for u in range(1, EARLY):
+            load_block(u)
         nc.sync.dma_start(out=w_words[:].bitcast(I32), in_=W_words[0].bitcast(I32))
         for q in range(QUADRANTS):
             nc.sync.dma_start(
                 out=w_scales[QUAD * q : QUAD * q + QUAD_SCALES, :].bitcast(I32),
                 in_=W_scales[0, QUAD_SCALES * q : QUAD_SCALES * (q + 1), :].bitcast(I32),
             )
-        for u in range(2, NUNITS):
-            load_unit(u)
+        for u in range(EARLY, NBLOCKS):
+            load_block(u)
 
         ident = const.tile([P, P], F32)
         make_identity(nc, ident[:])
@@ -101,116 +100,141 @@ def tile_linearnnencoder_kernel(tc, x, W_words, W_scales, b, out):
         ident_bf = const.tile([P, NARROW], BF16)
         nc.vector.tensor_copy(out=ident_bf[:], in_=ident[:, 0:NARROW])
 
-        b_ps = acc_psum.tile([P, NARROW], F32, tag="acc")
-        nc.tensor.matmul(out=b_ps[:], lhsT=b_top[:], rhs=ident_bf[:], start=True, stop=True)
         b_col = const.tile([P, CHUNKS], F32)
-        nc.vector.tensor_copy(out=b_col[:], in_=b_ps[:, 0:CHUNKS])
+
+        def place_bias():
+            b_ps = acc_psum.tile([P, NARROW], F32, tag="acc")
+            nc.tensor.matmul(out=b_ps[:], lhsT=b_top[:], rhs=ident_bf[:], start=True, stop=True)
+            nc.scalar.copy(out=b_col[:], in_=b_ps[:, 0:CHUNKS])
 
         any_differs = const.tile([P, NTILES], F32)
         stats = const.tile([P, CHUNKS, 3, SAMPLES], F32)
 
+        flags = {}
         row_masks = {}
+        groups = {}
         quantised = {}
         sums = {}
+        outputs = {}
 
-        def test_rows(u):
-            first, n = UNIT_START[u], UNIT_TILES[u]
-            on_scalar = SCALAR_TESTS if n == TILES else 0
-            on_vector = n - on_scalar
-            x_words = x_units[u][:].bitcast(F32)
-            differs = work.tile([P, on_vector, WORDS], BF16, name="differs")
+        def flag_words(u):
+            differs = work.tile([P, ON_VECTOR, WORDS], BF16, name="differs")
             nc.vector.tensor_single_scalar(
-                out=differs[:], in_=x_words[:, 0:on_vector, :], scalar=PAD_WORD, op=ALU.not_equal
+                out=differs[:], in_=x_blocks[u][:].bitcast(F32)[:, 0:ON_VECTOR, :], scalar=PAD_WORD, op=ALU.not_equal
             )
+            flags[u] = differs
+
+        def join_flags(u):
             nc.vector.tensor_reduce(
-                out=any_differs[:, first : first + on_vector],
-                in_=differs[:].bitcast(I32),
+                out=any_differs[:, u * TILES : u * TILES + ON_VECTOR],
+                in_=flags[u][:].bitcast(I32),
                 axis=mybir.AxisListType.X,
                 op=ALU.max,
             )
-            for i in range(on_vector, n):
-                distance = work.tile([P, WORDS], BF16, name="distance")
-                nc.scalar.activation(
-                    out=distance[:],
-                    in_=x_words[:, i, :],
-                    func=ACT.Abs,
-                    bias=minus_pad_word[:, 0:1],
-                    accum_out=any_differs[:, first + i : first + i + 1],
-                )
-            mask = mask_pool.tile([P, n, P], F32, name="mask")
-            for i in range(n):
-                t = first + i
+
+        def test_on_scalar(u, i):
+            distance = work.tile([P, WORDS], BF16, name="distance")
+            nc.scalar.activation(
+                out=distance[:],
+                in_=x_blocks[u][:].bitcast(F32)[:, i, :],
+                func=ACT.Abs,
+                bias=minus_pad_word[:, 0:1],
+                accum_out=any_differs[:, u * TILES + i : u * TILES + i + 1],
+            )
+
+        def make_masks(u, tiles):
+            if u not in row_masks:
+                mask = mask_pool.tile([P, TILES, P], F32, name="mask")
+                row_masks[u] = mask
+            for i in tiles:
+                t = u * TILES + i
                 nc.vector.tensor_scalar(
-                    out=mask[:, i, :],
+                    out=row_masks[u][:, i, :],
                     in0=ident[:],
                     scalar1=any_differs[:, t : t + 1],
                     scalar2=0.0,
                     op0=ALU.mult,
                     op1=ALU.is_gt,
                 )
-            row_masks[u] = mask
 
-        def flip(u):
-            n = UNIT_TILES[u]
-            x_words = x_units[u][:].bitcast(F32)
-            grouped = work.tile([P, 4 * n * P], BF16, name="grouped", align_bytes=64)
-            grouped_words = grouped[:].bitcast(F32)
-            for start in range(0, n, 2):
-                m = min(2, n - start)
-                planes = flip_psum.tile([P, 2, m * P], F32, name="planes")
-                for j in range(m):
-                    for w in range(2):
-                        nc.tensor.transpose(
-                            planes[:, w, j * P : (j + 1) * P], x_words[:, start + j, w:WORDS:2], row_masks[u][:, start + j, :]
-                        )
-                nc.scalar.copy(
-                    out=grouped_words[:, 2 * start * P : 2 * (start + m) * P].rearrange("p (r w) -> p r w", w=2),
-                    in_=planes[:].rearrange("p w r -> p r w"),
-                )
-            x_codes = work.tile([P, n * P], U32, name="x_codes", align_bytes=64)
-            x_scales = work.tile([P, n * P], U8, name="x_scales", align_bytes=64)
-            nc.vector.quantize_mx(out=x_codes[:].bitcast(FP8X4), scales=x_scales[:], in_=grouped[:])
+        planes_of = {}
+
+        def flip(u, half):
+            x_words = x_blocks[u][:].bitcast(F32)
+            planes = flip_psum.tile([P, 2, 2 * P], F32, name="planes")
+            for j in range(2):
+                for w in range(2):
+                    nc.tensor.transpose(
+                        planes[:, w, j * P : (j + 1) * P],
+                        x_words[:, 2 * half + j, w:WORDS:2],
+                        row_masks[u][:, 2 * half + j, :],
+                    )
+            planes_of[u, half] = planes
+
+        def group(u, half):
+            if u not in groups:
+                grouped = work.tile([P, 4 * BLOCK], BF16, name="grouped", align_bytes=64)
+                groups[u] = grouped
+            grouped_words = groups[u][:].bitcast(F32)
+            nc.scalar.copy(
+                out=grouped_words[:, half * BLOCK : (half + 1) * BLOCK].rearrange("p (r w) -> p r w", w=2),
+                in_=planes_of[u, half][:].rearrange("p w r -> p r w"),
+            )
+
+        def quantise(u):
+            x_codes = work.tile([P, BLOCK], U32, name="x_codes", align_bytes=64)
+            x_scales = work.tile([P, BLOCK], U8, name="x_scales", align_bytes=64)
+            nc.vector.quantize_mx(out=x_codes[:].bitcast(FP8X4), scales=x_scales[:], in_=groups[u][:])
             quantised[u] = (x_codes, x_scales)
 
-        def multiply(u):
+        def multiply(u, c):
             x_codes, x_scales = quantised[u]
-            for c in range(CHUNKS):
-                acc = acc_psum.tile([P, UNIT_TILES[u] * P], F32, name="acc")
-                nc.tensor.matmul_mx(
-                    out=acc[:],
-                    lhsT=w_words[:, 2 * c * P : 2 * (c + 1) * P].bitcast(FP4X4),
-                    lhsT_scale=w_scales[:, c * P : (c + 1) * P],
-                    rhs=x_codes[:].bitcast(FP8X4),
-                    rhs_scale=x_scales[:],
-                    start=True,
-                    stop=True,
-                )
-                sums[c] = acc
+            acc = acc_psum.tile([P, BLOCK], F32, name="acc")
+            nc.tensor.matmul_mx(
+                out=acc[:],
+                lhsT=w_words[:, 2 * c * P : 2 * (c + 1) * P].bitcast(FP4X4),
+                lhsT_scale=w_scales[:, c * P : (c + 1) * P],
+                rhs=x_codes[:].bitcast(FP8X4),
+                rhs_scale=x_scales[:],
+                start=True,
+                stop=True,
+            )
+            sums[c] = acc
 
         def activate(u, c):
-            y = y_pool.tile([P, UNIT_TILES[u] * P], F32, name="y")
+            y = y_pool.tile([P, BLOCK], F32, name="y")
             nc.scalar.activation(out=y[:], in_=sums[c][:], func=ACT.Gelu, bias=b_col[:, c : c + 1])
-            for pair in range(UNIT_TILES[u] * TILE_SAMPLES // 2):
-                s = UNIT_START[u] * TILE_SAMPLES + 2 * pair
+            outputs[c] = y
+
+        def take_stats(u, c, pairs):
+            for pair in pairs:
+                s = u * BLOCK_SAMPLES + 2 * pair
                 nc.vector.bn_stats(
                     out=stats[:, c, :, s : s + 2].rearrange("p v s -> p s v"),
-                    in_=y[:, 2 * pair * TOKENS : 2 * (pair + 1) * TOKENS].rearrange("p (s t) -> p t s", s=2),
+                    in_=outputs[c][:, 2 * pair * TOKENS : 2 * (pair + 1) * TOKENS].rearrange("p (s t) -> p t s", s=2),
                 )
-            return y
 
+        valid = const.tile([P, NTILES], F32)
         spread = const.tile([P, NTILES, QUADRANTS], BF16)
         pad_y_col = const.tile([P, CHUNKS], F32)
+        minus_pad_y = const.tile([P, CHUNKS], F32)
+
+        def find_pad_y():
+            nc.scalar.activation(out=pad_y_col[:], in_=b_col[:], func=ACT.Gelu)
+            nc.gpsimd.tensor_scalar(
+                out=minus_pad_y[:], in0=pad_y_col[:], scalar1=-1.0, scalar2=0.0, op0=ALU.mult, op1=ALU.add
+            )
 
         def mark_valid_rows():
-            nc.vector.scalar_tensor_tensor(
-                out=spread[:],
-                in0=any_differs[:].unsqueeze(2).to_broadcast([P, NTILES, QUADRANTS]),
-                scalar=0.0,
-                in1=quadrant[:].unsqueeze(1).to_broadcast([P, NTILES, QUADRANTS]),
-                op0=ALU.is_gt,
-                op1=ALU.mult,
+            nc.gpsimd.tensor_scalar(
+                out=valid[:], in0=any_differs[:], scalar1=0.0, scalar2=1.0, op0=ALU.is_gt, op1=ALU.mult
             )
-            nc.scalar.activation(out=pad_y_col[:], in_=b_col[:], func=ACT.Gelu)
+            nc.gpsimd.tensor_tensor(
+                out=spread[:],
+                in0=valid[:].unsqueeze(2).to_broadcast([P, NTILES, QUADRANTS]),
+                in1=quadrant[:].unsqueeze(1).to_broadcast([P, NTILES, QUADRANTS]),
+                op=ALU.mult,
+            )
 
         stretch = const.tile([P, 1], F32)
         between = const.tile([P, 1], F32)
@@ -227,40 +251,50 @@ def tile_linearnnencoder_kernel(tc, x, W_words, W_scales, b, out):
                 nc.tensor.transpose(
                     pad_y_ps[:, c * P : (c + 1) * P], pad_y_col[:, c : c + 1].to_broadcast([P, P]), ident[:]
                 )
+            return n_ps, pad_y_ps
+
+        def derive_counts(n_ps, pad_y_ps):
             n = const.tile([P, 1], F32)
-            nc.vector.tensor_copy(out=n[:], in_=n_ps[:, 0:1])
-            inv_n = const.tile([P, 1], F32)
-            nc.vector.tensor_scalar_max(out=inv_n[:], in0=n[:], scalar1=1.0)
-            nc.vector.reciprocal(out=inv_n[:], in_=inv_n[:])
+            nc.scalar.copy(out=n[:], in_=n_ps[:, 0:1])
             some = const.tile([P, 1], F32)
-            nc.vector.tensor_scalar_min(out=some[:], in0=n[:], scalar1=1.0)
-            nc.vector.tensor_scalar(
+            nc.gpsimd.tensor_scalar(out=some[:], in0=n[:], scalar1=1.0, scalar2=1.0, op0=ALU.min, op1=ALU.mult)
+            at_least_1 = const.tile([P, 1], F32)
+            nc.gpsimd.tensor_scalar(out=at_least_1[:], in0=n[:], scalar1=1.0, scalar2=1.0, op0=ALU.max, op1=ALU.mult)
+            dof = const.tile([P, 1], F32)
+            nc.gpsimd.tensor_scalar(out=dof[:], in0=n[:], scalar1=-1.0, scalar2=1.0, op0=ALU.add, op1=ALU.max)
+            padding = const.tile([P, 1], F32)
+            nc.gpsimd.tensor_scalar(
+                out=padding[:], in0=n[:], scalar1=-float(TOKENS), scalar2=float(TOKENS), op0=ALU.add, op1=ALU.mult
+            )
+            nc.scalar.activation(out=pad_y_some[:], in_=pad_y_ps[:], func=ACT.Copy, scale=some[:, 0:1])
+            return n, some, at_least_1, dof, padding
+
+        def invert_counts(n, some, at_least_1, dof, padding):
+            inv_n = const.tile([P, 1], F32)
+            nc.vector.reciprocal(out=inv_n[:], in_=at_least_1[:])
+            inv_dof = const.tile([P, 1], F32)
+            nc.vector.reciprocal(out=inv_dof[:], in_=dof[:])
+            nc.gpsimd.tensor_scalar(
                 out=stretch[:], in0=inv_n[:], scalar1=float(TOKENS), scalar2=some[:, 0:1], op0=ALU.mult, op1=ALU.mult
             )
-            nc.vector.tensor_scalar(
-                out=between[:], in0=n[:], scalar1=-float(TOKENS), scalar2=float(TOKENS), op0=ALU.add, op1=ALU.mult
-            )
-            nc.vector.tensor_mul(out=between[:], in0=between[:], in1=inv_n[:])
-            inv_dof = const.tile([P, 1], F32)
-            nc.vector.tensor_scalar(out=inv_dof[:], in0=n[:], scalar1=-1.0, scalar2=1.0, op0=ALU.add, op1=ALU.max)
-            nc.vector.reciprocal(out=inv_dof[:], in_=inv_dof[:])
-            nc.vector.tensor_scalar(
+            nc.gpsimd.tensor_tensor(out=between[:], in0=padding[:], in1=inv_n[:], op=ALU.mult)
+            nc.gpsimd.tensor_scalar(
                 out=scale_var[:], in0=n[:], scalar1=1.0, scalar2=inv_dof[:, 0:1], op0=ALU.is_gt, op1=ALU.mult
             )
-            nc.vector.tensor_scalar_mul(out=pad_y_some[:], in0=pad_y_ps[:], scalar1=some[:, 0:1])
 
         turned = {}
         squares = {}
+        withins = {}
         result = const.tile([P, 2 * OUT], F32)
 
         def turn_chunk(c):
             d = ends.tile([P, SAMPLES], F32, name="d")
-            nc.vector.tensor_scalar(
-                out=d[:], in0=stats[:, c, 1, :], scalar1=pad_y_col[:, c : c + 1], scalar2=None, op0=ALU.subtract
+            nc.gpsimd.tensor_scalar(
+                out=d[:], in0=stats[:, c, 1, :], scalar1=1.0, scalar2=minus_pad_y[:, c : c + 1], op0=ALU.mult, op1=ALU.add
             )
-            d_m32_t = acc_psum.tile([P, 2, P], F32, tag="acc")
-            nc.tensor.transpose(d_m32_t[:, 0, :], d[:], ident[:])
+            d_m32_t = flip_psum.tile([P, 2, P], F32, tag="planes")
             nc.tensor.transpose(d_m32_t[:, 1, :], stats[:, c, 2, :], ident[:])
+            nc.tensor.transpose(d_m32_t[:, 0, :], d[:], ident[:])
             turned[c] = d_m32_t
 
         def square_chunk(c):
@@ -268,46 +302,136 @@ def tile_linearnnencoder_kernel(tc, x, W_words, W_scales, b, out):
             nc.scalar.activation(out=square[:], in_=turned[c][:, 0, :], func=ACT.Square)
             squares[c] = square
 
-        def finish_chunk(c):
-            d_m32_t = turned[c]
-            cols = slice(c * P, (c + 1) * P)
-            within = ends.tile([P, P], F32, name="within")
-            nc.vector.scalar_tensor_tensor(
-                out=within[:], in0=squares[c][:], scalar=between[:, 0:1], in1=d_m32_t[:, 1, :], op0=ALU.mult, op1=ALU.add
-            )
-            nc.vector.tensor_scalar_max(out=within[:], in0=within[:], scalar1=0.0)
+        def finish_mean(c):
             nc.vector.scalar_tensor_tensor(
                 out=result[:, OUT + c * P : OUT + (c + 1) * P],
-                in0=d_m32_t[:, 0, :],
+                in0=turned[c][:, 0, :],
                 scalar=stretch[:, 0:1],
-                in1=pad_y_some[:, cols],
+                in1=pad_y_some[:, c * P : (c + 1) * P],
                 op0=ALU.mult,
                 op1=ALU.add,
             )
-            nc.scalar.activation(out=result[:, cols], in_=within[:], func=ACT.Sqrt, scale=scale_var[:, 0:1])
 
-        test_rows(0)
-        flip(0)
-        for u in range(1, AHEAD):
-            test_rows(u)
-        for u in range(NUNITS):
-            if u + AHEAD < NUNITS:
-                test_rows(u + AHEAD)
-            if u + AHEAD == NUNITS:
+        def finish_sum(c):
+            within = ends.tile([P, P], F32, name="within")
+            nc.vector.scalar_tensor_tensor(
+                out=within[:],
+                in0=squares[c][:],
+                scalar=between[:, 0:1],
+                in1=turned[c][:, 1, :],
+                op0=ALU.mult,
+                op1=ALU.add,
+            )
+            withins[c] = within
+
+        def clip_sum(c):
+            nc.vector.tensor_scalar_max(out=withins[c][:], in0=withins[c][:], scalar1=0.0)
+
+        def root_chunk(c):
+            nc.scalar.activation(
+                out=result[:, c * P : (c + 1) * P], in_=withins[c][:], func=ACT.Sqrt, scale=scale_var[:, 0:1]
+            )
+
+        all_pairs = range(PAIRS)
+        front, back = range(PAIRS // 2), range(PAIRS // 2, PAIRS)
+
+        def test_on_both(u):
+            flag_words(u)
+            for i in range(ON_VECTOR, TILES):
+                test_on_scalar(u, i)
+            join_flags(u)
+
+        for u in range(2):
+            test_on_both(u)
+            make_masks(u, range(TILES))
+            flip(u, 0)
+            flip(u, 1)
+        test_on_both(2)
+        group(0, 0)
+        group(0, 1)
+        make_masks(2, range(TILES))
+        test_on_both(3)
+        quantise(0)
+        group(1, 0)
+        place_bias()
+        make_masks(3, range(TILES))
+        multiply(0, 0)
+        flip(2, 0)
+        flip(2, 1)
+        for c in range(1, CHUNKS):
+            multiply(0, c)
+        test_on_both(4)
+        group(1, 1)
+        find_pad_y()
+
+        for u in range(NBLOCKS - 1):
+            nxt, copied, turn, mask, test = u + 1, u + 2, u + 3, u + 4, u + AHEAD
+            quantise(nxt)
+            if test < NBLOCKS:
+                flag_words(test)
+            activate(u, 0)
+            if copied < NBLOCKS:
+                group(copied, 0)
+            take_stats(u, 0, front)
+            if test < NBLOCKS:
+                join_flags(test)
+            take_stats(u, 0, back)
+            multiply(nxt, 0)
+            if turn < NBLOCKS:
+                flip(turn, 0)
+                flip(turn, 1)
+            activate(u, 1)
+            if copied < NBLOCKS:
+                group(copied, 1)
+            take_stats(u, 1, front)
+            if mask < NBLOCKS:
+                make_masks(mask, range(TILES))
+            take_stats(u, 1, back)
+            multiply(nxt, 1)
+            if u == NBLOCKS - 3:
+                count_banks = count_valid_rows()
+            activate(u, 2)
+            if test < NBLOCKS:
+                test_on_scalar(test, 2)
+            take_stats(u, 2, all_pairs)
+            multiply(nxt, 2)
+            activate(u, 3)
+            if test < NBLOCKS:
+                test_on_scalar(test, 3)
+            take_stats(u, 3, all_pairs)
+            multiply(nxt, 3)
+            if u == NBLOCKS - 4:
                 mark_valid_rows()
-            if u + 1 < NUNITS:
-                flip(u + 1)
-            if u + 1 == NUNITS:
-                count_valid_rows()
-            multiply(u)
-            for c in range(CHUNKS):
-                last_y = activate(u, c)
-                if u + 1 == NUNITS:
-                    turn_chunk(c)
-        nc.scalar.activation(out=warm[:], in_=last_y[:, 0:1], func=ACT.Sqrt, scale=0.0, bias=one[:, 0:1])
+            if u == NBLOCKS - 3:
+                counts = derive_counts(*count_banks)
+
+        u = NBLOCKS - 1
+        invert_counts(*counts)
         for c in range(CHUNKS):
-            square_chunk(c)
+            activate(u, c)
+        nc.scalar.activation(out=warm[:], in_=one[:], func=ACT.Sqrt)
         for c in range(CHUNKS):
-            finish_chunk(c)
+            take_stats(u, c, all_pairs)
+            turn_chunk(c)
+            if c < CHUNKS - 1:
+                square_chunk(c)
+        finish_sum(0)
+        finish_sum(1)
+        clip_sum(0)
+        finish_sum(2)
+        clip_sum(1)
+        root_chunk(0)
+        square_chunk(3)
+        finish_mean(0)
+        clip_sum(2)
+        root_chunk(1)
+        root_chunk(2)
+        nc.sync.dma_start(out=out[:, 0 : 3 * P], in_=result[:, 0 : 3 * P])
+        finish_mean(1)
+        finish_mean(2)
+        finish_sum(3)
+        finish_mean(3)
+        clip_sum(3)
+        root_chunk(3)
         nc.sync.dma_start(out=out[:, OUT : 2 * OUT], in_=result[:, OUT : 2 * OUT])
-        nc.sync.dma_start(out=out[:, 0:OUT], in_=result[:, 0:OUT])
+        nc.scalar.dma_start(out=out[:, 3 * P : OUT], in_=result[:, 3 * P : OUT])

@@ -30,6 +30,8 @@ assert TOKENS == QUAD
 QUAD_SCALES = QUAD // 8
 WORDS = K // 2
 PAD_WORD = -(1.0 + 0xBF80 / 2.0**23)
+MAGNIFY = 2.0**24
+FIRST_ON_GPSIMD = 4
 TILE_SAMPLES = P // TOKENS
 PAIRS = BLOCK_SAMPLES // 2
 ON_VECTOR = 2
@@ -88,7 +90,7 @@ def tile_linearnnencoder_kernel(tc, x, W_words, W_scales, b, out):
         one = const.tile([P, 1], F32)
         nc.vector.memset(one[:], 1.0)
         minus_pad_word = const.tile([P, 1], F32)
-        nc.vector.memset(minus_pad_word[:], -PAD_WORD)
+        nc.vector.memset(minus_pad_word[:], -PAD_WORD * MAGNIFY)
         warm = const.tile([P, 1], F32)
         nc.scalar.activation(out=warm[:], in_=one[:], func=ACT.Gelu)
         ones = const.tile([P, NARROW], BF16)
@@ -139,6 +141,7 @@ def tile_linearnnencoder_kernel(tc, x, W_words, W_scales, b, out):
                 in_=x_blocks[u][:].bitcast(F32)[:, i, :],
                 func=ACT.Abs,
                 bias=minus_pad_word[:, 0:1],
+                scale=MAGNIFY,
                 accum_out=any_differs[:, u * TILES + i : u * TILES + i + 1],
             )
 
@@ -148,13 +151,14 @@ def tile_linearnnencoder_kernel(tc, x, W_words, W_scales, b, out):
                 row_masks[u] = mask
             for i in tiles:
                 t = u * TILES + i
-                nc.vector.tensor_scalar(
+                engine = nc.vector if u < FIRST_ON_GPSIMD else nc.gpsimd
+                engine.tensor_scalar(
                     out=row_masks[u][:, i, :],
                     in0=ident[:],
                     scalar1=any_differs[:, t : t + 1],
                     scalar2=0.0,
-                    op0=ALU.mult,
-                    op1=ALU.is_gt,
+                    op0=ALU.min,
+                    op1=ALU.max,
                 )
 
         planes_of = {}

@@ -26,7 +26,7 @@ NTILES = NBLOCKS * TILES
 BLOCK_SAMPLES = BLOCK // TOKENS
 QUAD = 32
 QUADRANTS = P // QUAD
-assert TOKENS == QUAD
+assert TOKENS % TILES == 0
 QUAD_SCALES = QUAD // 8
 WORDS = K // 2
 PAD_WORD = -(1.0 + 0xBF80 / 2.0**23)
@@ -68,7 +68,7 @@ def tile_linearnnencoder_kernel(tc, x, W_words, W_scales, b, out):
         def load_block(u):
             x_block = x_pool.tile([P, TILES, K], BF16, name="x_block")
             nc.sync.dma_start(
-                out=x_block[:], in_=x_rows[u * BLOCK : (u + 1) * BLOCK, :].rearrange("(i p) k -> p i k", p=P)
+                out=x_block[:], in_=x_rows[u * BLOCK : (u + 1) * BLOCK, :].rearrange("(p i) k -> p i k", i=TILES)
             )
             x_blocks.append(x_block)
 
@@ -95,10 +95,13 @@ def tile_linearnnencoder_kernel(tc, x, W_words, W_scales, b, out):
         nc.scalar.activation(out=warm[:], in_=one[:], func=ACT.Gelu)
         ones = const.tile([P, NARROW], BF16)
         nc.vector.memset(ones[:], 1.0)
-        quadrant = const.tile([P, QUADRANTS], F32)
-        nc.vector.memset(quadrant[:], 0.0)
-        for q in range(QUADRANTS):
-            nc.vector.memset(quadrant[QUAD * q : QUAD * (q + 1), q : q + 1], 1.0)
+        owner = const.tile([P, BLOCK_SAMPLES], F32)
+        nc.vector.tensor_reduce(
+            out=owner[:],
+            in_=ident[:].rearrange("p (q j) -> p q j", q=BLOCK_SAMPLES),
+            axis=mybir.AxisListType.X,
+            op=ALU.add,
+        )
         ident_bf = const.tile([P, NARROW], BF16)
         nc.vector.tensor_copy(out=ident_bf[:], in_=ident[:, 0:NARROW])
 
@@ -215,11 +218,14 @@ def tile_linearnnencoder_kernel(tc, x, W_words, W_scales, b, out):
                 s = u * BLOCK_SAMPLES + 2 * pair
                 nc.vector.bn_stats(
                     out=stats[:, c, :, s : s + 2].rearrange("p v s -> p s v"),
-                    in_=outputs[c][:, 2 * pair * TOKENS : 2 * (pair + 1) * TOKENS].rearrange("p (s t) -> p t s", s=2),
+                    in_=outputs[c][:].rearrange("p (i q j) -> p i j q", i=TILES, q=BLOCK_SAMPLES)[
+                        :, :, :, 2 * pair : 2 * pair + 2
+                    ],
                 )
 
         valid = const.tile([P, NTILES], F32)
-        spread = const.tile([P, NTILES, QUADRANTS], BF16)
+        valid_rows = const.tile([P, NBLOCKS], F32)
+        spread = const.tile([P, NBLOCKS, BLOCK_SAMPLES], BF16)
         pad_y_col = const.tile([P, CHUNKS], F32)
         minus_pad_y = const.tile([P, CHUNKS], F32)
 
@@ -233,10 +239,16 @@ def tile_linearnnencoder_kernel(tc, x, W_words, W_scales, b, out):
             nc.gpsimd.tensor_scalar(
                 out=valid[:], in0=any_differs[:], scalar1=0.0, scalar2=1.0, op0=ALU.is_gt, op1=ALU.mult
             )
+            nc.vector.tensor_reduce(
+                out=valid_rows[:],
+                in_=valid[:].rearrange("p (u i) -> p u i", i=TILES),
+                axis=mybir.AxisListType.X,
+                op=ALU.add,
+            )
             nc.gpsimd.tensor_tensor(
                 out=spread[:],
-                in0=valid[:].unsqueeze(2).to_broadcast([P, NTILES, QUADRANTS]),
-                in1=quadrant[:].unsqueeze(1).to_broadcast([P, NTILES, QUADRANTS]),
+                in0=valid_rows[:].unsqueeze(2).to_broadcast([P, NBLOCKS, BLOCK_SAMPLES]),
+                in1=owner[:].unsqueeze(1).to_broadcast([P, NBLOCKS, BLOCK_SAMPLES]),
                 op=ALU.mult,
             )
 
@@ -248,7 +260,7 @@ def tile_linearnnencoder_kernel(tc, x, W_words, W_scales, b, out):
         def count_valid_rows():
             n_ps = flip_psum.tile([P, NARROW], F32, tag="planes")
             nc.tensor.matmul(
-                out=n_ps[:], lhsT=spread[:].rearrange("p i q -> p (i q)"), rhs=ones[:], start=True, stop=True
+                out=n_ps[:], lhsT=spread[:].rearrange("p u q -> p (u q)"), rhs=ones[:], start=True, stop=True
             )
             pad_y_ps = flip_psum.tile([P, OUT], F32, tag="planes")
             for c in range(CHUNKS):

@@ -34,7 +34,7 @@ MAGNIFY = 2.0**24
 FIRST_ON_GPSIMD = 4
 TILE_SAMPLES = P // TOKENS
 PAIRS = BLOCK_SAMPLES // 2
-ON_VECTOR = 2
+VECTOR_TESTS = (2, 2, 2, 2, 2, 4, 2, 2)
 AHEAD = 5
 EARLY = 4
 NARROW = 32
@@ -115,6 +115,9 @@ def tile_linearnnencoder_kernel(tc, x, W_words, W_scales, b, out):
         any_differs = const.tile([P, NTILES], F32)
         stats = const.tile([P, CHUNKS, 3, SAMPLES], F32)
 
+        def vector_tests(u):
+            return VECTOR_TESTS[u]
+
         flags = {}
         row_masks = {}
         groups = {}
@@ -123,15 +126,16 @@ def tile_linearnnencoder_kernel(tc, x, W_words, W_scales, b, out):
         outputs = {}
 
         def flag_words(u):
-            differs = work.tile([P, ON_VECTOR, WORDS], BF16, name="differs")
+            on_vector = vector_tests(u)
+            differs = work.tile([P, on_vector, WORDS], BF16, name="differs")
             nc.vector.tensor_single_scalar(
-                out=differs[:], in_=x_blocks[u][:].bitcast(F32)[:, 0:ON_VECTOR, :], scalar=PAD_WORD, op=ALU.not_equal
+                out=differs[:], in_=x_blocks[u][:].bitcast(F32)[:, 0:on_vector, :], scalar=PAD_WORD, op=ALU.not_equal
             )
             flags[u] = differs
 
         def join_flags(u):
             nc.vector.tensor_reduce(
-                out=any_differs[:, u * TILES : u * TILES + ON_VECTOR],
+                out=any_differs[:, u * TILES : u * TILES + vector_tests(u)],
                 in_=flags[u][:].bitcast(I32),
                 axis=mybir.AxisListType.X,
                 op=ALU.max,
@@ -282,10 +286,10 @@ def tile_linearnnencoder_kernel(tc, x, W_words, W_scales, b, out):
             nc.gpsimd.tensor_scalar(
                 out=padding[:], in0=n[:], scalar1=-float(TOKENS), scalar2=float(TOKENS), op0=ALU.add, op1=ALU.mult
             )
-            nc.scalar.activation(out=pad_y_some[:], in_=pad_y_ps[:], func=ACT.Copy, scale=some[:, 0:1])
-            return n, some, at_least_1, dof, padding
+            return pad_y_ps, n, some, at_least_1, dof, padding
 
-        def invert_counts(n, some, at_least_1, dof, padding):
+        def invert_counts(pad_y_ps, n, some, at_least_1, dof, padding):
+            nc.scalar.activation(out=pad_y_some[:], in_=pad_y_ps[:], func=ACT.Copy, scale=some[:, 0:1])
             inv_n = const.tile([P, 1], F32)
             nc.vector.reciprocal(out=inv_n[:], in_=at_least_1[:])
             inv_dof = const.tile([P, 1], F32)
@@ -353,7 +357,7 @@ def tile_linearnnencoder_kernel(tc, x, W_words, W_scales, b, out):
 
         def test_on_both(u):
             flag_words(u)
-            for i in range(ON_VECTOR, TILES):
+            for i in range(vector_tests(u), TILES):
                 test_on_scalar(u, i)
             join_flags(u)
 
@@ -372,10 +376,11 @@ def tile_linearnnencoder_kernel(tc, x, W_words, W_scales, b, out):
         place_bias()
         make_masks(3, range(TILES))
         multiply(0, 0)
+        multiply(0, 1)
         flip(2, 0)
         flip(2, 1)
-        for c in range(1, CHUNKS):
-            multiply(0, c)
+        multiply(0, 2)
+        multiply(0, 3)
         test_on_both(4)
         group(1, 1)
         find_pad_y()
@@ -408,11 +413,12 @@ def tile_linearnnencoder_kernel(tc, x, W_words, W_scales, b, out):
                 count_banks = count_valid_rows()
             activate(u, 2)
             if test < NBLOCKS:
-                test_on_scalar(test, 2)
+                for i in range(vector_tests(test), TILES - 1):
+                    test_on_scalar(test, i)
             take_stats(u, 2, all_pairs)
             multiply(nxt, 2)
             activate(u, 3)
-            if test < NBLOCKS:
+            if test < NBLOCKS and vector_tests(test) < TILES:
                 test_on_scalar(test, 3)
             take_stats(u, 3, all_pairs)
             multiply(nxt, 3)

@@ -34,7 +34,7 @@ MAGNIFY = 2.0**24
 FIRST_ON_GPSIMD = 4
 TILE_SAMPLES = P // TOKENS
 PAIRS = BLOCK_SAMPLES // 2
-VECTOR_TESTS = (2, 2, 2, 2, 2, 4, 2, 2)
+VECTOR_TESTS = (2, 2, 2, 2, 3, 3, 2, 1)
 AHEAD = 5
 EARLY = 4
 NARROW = 32
@@ -111,6 +111,9 @@ def tile_linearnnencoder_kernel(tc, x, W_words, W_scales, b, out):
             b_ps = acc_psum.tile([P, NARROW], F32, tag="acc")
             nc.tensor.matmul(out=b_ps[:], lhsT=b_top[:], rhs=ident_bf[:], start=True, stop=True)
             nc.scalar.copy(out=b_col[:], in_=b_ps[:, 0:CHUNKS])
+
+        minus_ones = const.tile([P, P], F32)
+        nc.gpsimd.memset(minus_ones[:], -1.0)
 
         any_differs = const.tile([P, NTILES], F32)
         stats = const.tile([P, CHUNKS, 3, SAMPLES], F32)
@@ -231,13 +234,16 @@ def tile_linearnnencoder_kernel(tc, x, W_words, W_scales, b, out):
         valid_rows = const.tile([P, NBLOCKS], F32)
         spread = const.tile([P, NBLOCKS, BLOCK_SAMPLES], BF16)
         pad_y_col = const.tile([P, CHUNKS], F32)
-        minus_pad_y = const.tile([P, CHUNKS], F32)
+        pad_y_diag = const.tile([P, CHUNKS, P], F32)
 
         def find_pad_y():
             nc.scalar.activation(out=pad_y_col[:], in_=b_col[:], func=ACT.Gelu)
-            nc.gpsimd.tensor_scalar(
-                out=minus_pad_y[:], in0=pad_y_col[:], scalar1=-1.0, scalar2=0.0, op0=ALU.mult, op1=ALU.add
-            )
+
+        def lay_out_pad_y():
+            for c in range(CHUNKS):
+                nc.gpsimd.tensor_scalar(
+                    out=pad_y_diag[:, c, :], in0=ident[:], scalar1=pad_y_col[:, c : c + 1], scalar2=0.0, op0=ALU.mult, op1=ALU.add
+                )
 
         def mark_valid_rows():
             nc.gpsimd.tensor_scalar(
@@ -289,7 +295,6 @@ def tile_linearnnencoder_kernel(tc, x, W_words, W_scales, b, out):
             return pad_y_ps, n, some, at_least_1, dof, padding
 
         def invert_counts(pad_y_ps, n, some, at_least_1, dof, padding):
-            nc.scalar.activation(out=pad_y_some[:], in_=pad_y_ps[:], func=ACT.Copy, scale=some[:, 0:1])
             inv_n = const.tile([P, 1], F32)
             nc.vector.reciprocal(out=inv_n[:], in_=at_least_1[:])
             inv_dof = const.tile([P, 1], F32)
@@ -301,31 +306,37 @@ def tile_linearnnencoder_kernel(tc, x, W_words, W_scales, b, out):
             nc.gpsimd.tensor_scalar(
                 out=scale_var[:], in0=n[:], scalar1=1.0, scalar2=inv_dof[:, 0:1], op0=ALU.is_gt, op1=ALU.mult
             )
+            return pad_y_ps, some
+
+        def spread_pad_y(pad_y_ps, some):
+            nc.scalar.activation(out=pad_y_some[:], in_=pad_y_ps[:], func=ACT.Copy, scale=some[:, 0:1])
 
         turned = {}
+        m32_turned = {}
         squares = {}
         withins = {}
         result = const.tile([P, 2 * OUT], F32)
 
+        def open_chunk(c):
+            d_t = acc_psum.tile([P, P], F32, tag="acc")
+            nc.tensor.matmul(out=d_t[:], lhsT=minus_ones[:], rhs=pad_y_diag[:, c, :], start=True, stop=False)
+            turned[c] = d_t
+
         def turn_chunk(c):
-            d = ends.tile([P, SAMPLES], F32, name="d")
-            nc.gpsimd.tensor_scalar(
-                out=d[:], in0=stats[:, c, 1, :], scalar1=1.0, scalar2=minus_pad_y[:, c : c + 1], op0=ALU.mult, op1=ALU.add
-            )
-            d_m32_t = flip_psum.tile([P, 2, P], F32, tag="planes")
-            nc.tensor.transpose(d_m32_t[:, 1, :], stats[:, c, 2, :], ident[:])
-            nc.tensor.transpose(d_m32_t[:, 0, :], d[:], ident[:])
-            turned[c] = d_m32_t
+            nc.tensor.matmul(out=turned[c][:], lhsT=stats[:, c, 1, :], rhs=ident[:], start=False, stop=True)
+            m32_t = flip_psum.tile([P, P], F32, tag="planes")
+            nc.tensor.transpose(m32_t[:], stats[:, c, 2, :], ident[:])
+            m32_turned[c] = m32_t
 
         def square_chunk(c):
             square = ends.tile([P, P], F32, name="square")
-            nc.scalar.activation(out=square[:], in_=turned[c][:, 0, :], func=ACT.Square)
+            nc.scalar.activation(out=square[:], in_=turned[c][:], func=ACT.Square)
             squares[c] = square
 
         def finish_mean(c):
             nc.vector.scalar_tensor_tensor(
                 out=result[:, OUT + c * P : OUT + (c + 1) * P],
-                in0=turned[c][:, 0, :],
+                in0=turned[c][:],
                 scalar=stretch[:, 0:1],
                 in1=pad_y_some[:, c * P : (c + 1) * P],
                 op0=ALU.mult,
@@ -338,7 +349,7 @@ def tile_linearnnencoder_kernel(tc, x, W_words, W_scales, b, out):
                 out=within[:],
                 in0=squares[c][:],
                 scalar=between[:, 0:1],
-                in1=turned[c][:, 1, :],
+                in1=m32_turned[c][:],
                 op0=ALU.mult,
                 op1=ALU.add,
             )
@@ -355,43 +366,58 @@ def tile_linearnnencoder_kernel(tc, x, W_words, W_scales, b, out):
         all_pairs = range(PAIRS)
         front, back = range(PAIRS // 2), range(PAIRS // 2, PAIRS)
 
+        def scalar_tests(u):
+            for i in range(vector_tests(u), TILES):
+                test_on_scalar(u, i)
+
         def test_on_both(u):
             flag_words(u)
             for i in range(vector_tests(u), TILES):
                 test_on_scalar(u, i)
             join_flags(u)
 
-        for u in range(2):
-            test_on_both(u)
-            make_masks(u, range(TILES))
-            flip(u, 0)
-            flip(u, 1)
-        test_on_both(2)
+        test_on_both(0)
+        make_masks(0, range(TILES))
+        flip(0, 0)
+        flip(0, 1)
+        test_on_both(1)
+        scalar_tests(2)
+        flag_words(2)
+        make_masks(1, range(TILES))
+        flip(1, 0)
+        flip(1, 1)
         group(0, 0)
         group(0, 1)
+        join_flags(2)
+        flag_words(3)
+        scalar_tests(3)
         make_masks(2, range(TILES))
-        test_on_both(3)
+        join_flags(3)
         quantise(0)
         group(1, 0)
         place_bias()
+        flag_words(4)
         make_masks(3, range(TILES))
+        join_flags(4)
         multiply(0, 0)
         multiply(0, 1)
         flip(2, 0)
         flip(2, 1)
         multiply(0, 2)
         multiply(0, 3)
-        test_on_both(4)
+        scalar_tests(4)
         group(1, 1)
         find_pad_y()
 
         for u in range(NBLOCKS - 1):
             nxt, copied, turn, mask, test = u + 1, u + 2, u + 3, u + 4, u + AHEAD
+            if u == 0:
+                flag_words(test)
             quantise(nxt)
-            if test < NBLOCKS:
+            if 0 < u and test < NBLOCKS:
                 flag_words(test)
             activate(u, 0)
-            if copied < NBLOCKS:
+            if 0 < u and copied < NBLOCKS:
                 group(copied, 0)
             take_stats(u, 0, front)
             if test < NBLOCKS:
@@ -402,6 +428,8 @@ def tile_linearnnencoder_kernel(tc, x, W_words, W_scales, b, out):
                 flip(turn, 0)
                 flip(turn, 1)
             activate(u, 1)
+            if u == 0:
+                group(copied, 0)
             if copied < NBLOCKS:
                 group(copied, 1)
             take_stats(u, 1, front)
@@ -424,36 +452,42 @@ def tile_linearnnencoder_kernel(tc, x, W_words, W_scales, b, out):
             multiply(nxt, 3)
             if u == NBLOCKS - 4:
                 mark_valid_rows()
+                lay_out_pad_y()
             if u == NBLOCKS - 3:
                 counts = derive_counts(*count_banks)
 
         u = NBLOCKS - 1
-        invert_counts(*counts)
+        pads = invert_counts(*counts)
         for c in range(CHUNKS):
             activate(u, c)
         nc.scalar.activation(out=warm[:], in_=one[:], func=ACT.Sqrt)
         for c in range(CHUNKS):
+            open_chunk(c)
+        for c in range(CHUNKS - 1):
             take_stats(u, c, all_pairs)
             turn_chunk(c)
-            if c < CHUNKS - 1:
-                square_chunk(c)
+            square_chunk(c)
+            if c == 1:
+                spread_pad_y(*pads)
+        take_stats(u, CHUNKS - 1, all_pairs)
+        turn_chunk(CHUNKS - 1)
         finish_sum(0)
         finish_sum(1)
         clip_sum(0)
         finish_sum(2)
         clip_sum(1)
-        root_chunk(0)
         square_chunk(3)
-        finish_mean(0)
         clip_sum(2)
+        root_chunk(0)
         root_chunk(1)
         root_chunk(2)
         nc.sync.dma_start(out=out[:, 0 : 3 * P], in_=result[:, 0 : 3 * P])
+        finish_mean(0)
         finish_mean(1)
-        finish_mean(2)
         finish_sum(3)
-        finish_mean(3)
+        finish_mean(2)
         clip_sum(3)
         root_chunk(3)
+        finish_mean(3)
         nc.sync.dma_start(out=out[:, OUT : 2 * OUT], in_=result[:, OUT : 2 * OUT])
         nc.scalar.dma_start(out=out[:, 3 * P : OUT], in_=result[:, 3 * P : OUT])

@@ -67,9 +67,12 @@ def tile_linearnnencoder_kernel(tc, x, W_words, W_scales, b, out):
 
         def load_block(u):
             x_block = x_pool.tile([P, TILES, K], BF16, name="x_block")
-            nc.sync.dma_start(
-                out=x_block[:], in_=x_rows[u * BLOCK : (u + 1) * BLOCK, :].rearrange("(p i) k -> p i k", i=TILES)
-            )
+            rows = x_rows[u * BLOCK : (u + 1) * BLOCK, :].rearrange("(p i) k -> p i k", i=TILES)
+            if u == 0:
+                for i in range(0, TILES, 2):
+                    nc.sync.dma_start(out=x_block[:, i : i + 2, :], in_=rows[:, i : i + 2, :])
+            else:
+                nc.sync.dma_start(out=x_block[:], in_=rows)
             x_blocks.append(x_block)
 
         load_block(0)
@@ -377,16 +380,17 @@ def tile_linearnnencoder_kernel(tc, x, W_words, W_scales, b, out):
             join_flags(u)
 
         test_on_both(0)
-        make_masks(0, range(TILES))
+        make_masks(0, range(2))
         flip(0, 0)
+        make_masks(0, range(2, TILES))
         flip(0, 1)
         test_on_both(1)
+        group(0, 0)
         scalar_tests(2)
         flag_words(2)
         make_masks(1, range(TILES))
         flip(1, 0)
         flip(1, 1)
-        group(0, 0)
         group(0, 1)
         join_flags(2)
         flag_words(3)
@@ -481,13 +485,15 @@ def tile_linearnnencoder_kernel(tc, x, W_words, W_scales, b, out):
         root_chunk(0)
         root_chunk(1)
         root_chunk(2)
-        nc.sync.dma_start(out=out[:, 0 : 3 * P], in_=result[:, 0 : 3 * P])
         finish_mean(0)
         finish_mean(1)
         finish_sum(3)
         finish_mean(2)
         clip_sum(3)
-        root_chunk(3)
         finish_mean(3)
-        nc.sync.dma_start(out=out[:, OUT : 2 * OUT], in_=result[:, OUT : 2 * OUT])
+        nc.sync.dma_start(out=out[:, OUT : OUT + 2 * P], in_=result[:, OUT : OUT + 2 * P])
+        nc.sync.dma_start(out=out[:, 0 : 3 * P], in_=result[:, 0 : 3 * P])
+        nc.sync.dma_start(out=out[:, OUT + 2 * P : OUT + 3 * P], in_=result[:, OUT + 2 * P : OUT + 3 * P])
+        nc.sync.dma_start(out=out[:, OUT + 3 * P : 2 * OUT], in_=result[:, OUT + 3 * P : 2 * OUT])
+        root_chunk(3)
         nc.scalar.dma_start(out=out[:, 3 * P : OUT], in_=result[:, 3 * P : OUT])

from contextlib import ExitStack

import concourse.mybir as mybir
from concourse.masks import make_identity

F32 = mybir.dt.float32
BF16 = mybir.dt.bfloat16
I32 = mybir.dt.int32
U32 = mybir.dt.uint32
U8 = mybir.dt.uint8
FP8X4 = mybir.dt.float8_e4m3fn_x4
FP4X4 = mybir.dt.float4_e2m1fn_x4
ALU = mybir.AluOpType
ACT = mybir.ActivationFunctionType

P = 128
SAMPLES = 128
TOKENS = 32
K = 512
OUT = 512
CHUNKS = OUT // P
BLOCK = 512
TILES = BLOCK // P
NBLOCKS = SAMPLES * TOKENS // BLOCK
NTILES = NBLOCKS * TILES
BLOCK_SAMPLES = BLOCK // TOKENS
QUAD = 32
QUADRANTS = P // QUAD
assert TOKENS % TILES == 0
QUAD_SCALES = QUAD // 8
WORDS = K // 2
PAD_WORD = -(1.0 + 0xBF80 / 2.0**23)
MAGNIFY = 2.0**24
FIRST_ON_GPSIMD = 4
TILE_SAMPLES = P // TOKENS
PAIRS = BLOCK_SAMPLES // 2
VECTOR_TESTS = (2, 2, 2, 2, 3, 3, 2, 1)
AHEAD = 5
EARLY = 4
NARROW = 32

FLOPS = 2 * SAMPLES * TOKENS * K * OUT


def tile_linearnnencoder_kernel(tc, x, W_words, W_scales, b, out):
    nc = tc.nc
    x_rows = x.rearrange("s t k -> (s t) k")

    with ExitStack() as ctx:
        const = ctx.enter_context(tc.tile_pool(name="const", bufs=1))
        x_pool = ctx.enter_context(tc.tile_pool(name="x_pool", bufs=NBLOCKS))
        work = ctx.enter_context(tc.tile_pool(name="work", bufs=3))
        mask_pool = ctx.enter_context(tc.tile_pool(name="mask_pool", bufs=AHEAD + 1))
        y_pool = ctx.enter_context(tc.tile_pool(name="y_pool", bufs=2 * CHUNKS))
        ends = ctx.enter_context(tc.tile_pool(name="ends", bufs=CHUNKS))
        flip_psum = ctx.enter_context(tc.psum_pool(name="flip_psum", bufs=4))
        acc_psum = ctx.enter_context(tc.psum_pool(name="acc_psum", bufs=CHUNKS))
        ctx.enter_context(tc.manual_schedule())

        w_words = const.tile([P, 2 * OUT], U8, align_bytes=64)
        w_scales = const.tile([P, OUT], U8, align_bytes=64)
        b_top = const.tile([P, P], BF16)
        nc.vector.memset(b_top[:], 0.0)
        nc.vector.memset(w_scales[:].bitcast(I32), 0)

        x_blocks = []

        def load_block(u):
            x_block = x_pool.tile([P, TILES, K], BF16, name="x_block")
            rows = x_rows[u * BLOCK : (u + 1) * BLOCK, :].rearrange("(p i) k -> p i k", i=TILES)
            if u == 0:
                for i in range(0, TILES, 2):
                    nc.sync.dma_start(out=x_block[:, i : i + 2, :], in_=rows[:, i : i + 2, :])
            else:
                nc.sync.dma_start(out=x_block[:], in_=rows)
            x_blocks.append(x_block)

        load_block(0)
        nc.sync.dma_start(out=b_top[0:CHUNKS, :], in_=b.rearrange("(c f) -> c f", f=P))
        for u in range(1, EARLY):
            load_block(u)
        nc.sync.dma_start(out=w_words[:].bitcast(I32), in_=W_words[0].bitcast(I32))
        for q in range(QUADRANTS):
            nc.sync.dma_start(
                out=w_scales[QUAD * q : QUAD * q + QUAD_SCALES, :].bitcast(I32),
                in_=W_scales[0, QUAD_SCALES * q : QUAD_SCALES * (q + 1), :].bitcast(I32),
            )
        for u in range(EARLY, NBLOCKS):
            load_block(u)

        ident = const.tile([P, P], F32)
        make_identity(nc, ident[:])
        one = const.tile([P, 1], F32)
        nc.vector.memset(one[:], 1.0)
        minus_pad_word = const.tile([P, 1], F32)
        nc.vector.memset(minus_pad_word[:], -PAD_WORD * MAGNIFY)
        warm = const.tile([P, 1], F32)
        nc.scalar.activation(out=warm[:], in_=one[:], func=ACT.Gelu)
        ones = const.tile([P, NARROW], BF16)
        nc.vector.memset(ones[:], 1.0)
        owner = const.tile([P, BLOCK_SAMPLES], F32)
        nc.vector.tensor_reduce(
            out=owner[:],
            in_=ident[:].rearrange("p (q j) -> p q j", q=BLOCK_SAMPLES),
            axis=mybir.AxisListType.X,
            op=ALU.add,
        )
        ident_bf = const.tile([P, NARROW], BF16)
        nc.vector.tensor_copy(out=ident_bf[:], in_=ident[:, 0:NARROW])

        b_col = const.tile([P, CHUNKS], F32)

        def place_bias():
            b_ps = acc_psum.tile([P, NARROW], F32, tag="acc")
            nc.tensor.matmul(out=b_ps[:], lhsT=b_top[:], rhs=ident_bf[:], start=True, stop=True)
            nc.scalar.copy(out=b_col[:], in_=b_ps[:, 0:CHUNKS])

        minus_ones = const.tile([P, P], F32)
        nc.gpsimd.memset(minus_ones[:], -1.0)

        any_differs = const.tile([P, NTILES], F32)
        stats = const.tile([P, CHUNKS, 3, SAMPLES], F32)

        def vector_tests(u):
            return VECTOR_TESTS[u]

        flags = {}
        row_masks = {}
        groups = {}
        quantised = {}
        sums = {}
        outputs = {}

        def flag_words(u):
            on_vector = vector_tests(u)
            differs = work.tile([P, on_vector, WORDS], BF16, name="differs")
            nc.vector.tensor_single_scalar(
                out=differs[:], in_=x_blocks[u][:].bitcast(F32)[:, 0:on_vector, :], scalar=PAD_WORD, op=ALU.not_equal
            )
            flags[u] = differs

        def join_flags(u):
            nc.vector.tensor_reduce(
                out=any_differs[:, u * TILES : u * TILES + vector_tests(u)],
                in_=flags[u][:].bitcast(I32),
                axis=mybir.AxisListType.X,
                op=ALU.max,
            )

        def test_on_scalar(u, i):
            distance = work.tile([P, WORDS], BF16, name="distance")
            nc.scalar.activation(
                out=distance[:],
                in_=x_blocks[u][:].bitcast(F32)[:, i, :],
                func=ACT.Abs,
                bias=minus_pad_word[:, 0:1],
                scale=MAGNIFY,
                accum_out=any_differs[:, u * TILES + i : u * TILES + i + 1],
            )

        def make_masks(u, tiles):
            if u not in row_masks:
                mask = mask_pool.tile([P, TILES, P], F32, name="mask")
                row_masks[u] = mask
            for i in tiles:
                t = u * TILES + i
                engine = nc.vector if u < FIRST_ON_GPSIMD else nc.gpsimd
                engine.tensor_scalar(
                    out=row_masks[u][:, i, :],
                    in0=ident[:],
                    scalar1=any_differs[:, t : t + 1],
                    scalar2=0.0,
                    op0=ALU.min,
                    op1=ALU.max,
                )

        planes_of = {}

        def flip(u, half):
            x_words = x_blocks[u][:].bitcast(F32)
            planes = flip_psum.tile([P, 2, 2 * P], F32, name="planes")
            for j in range(2):
                for w in range(2):
                    nc.tensor.transpose(
                        planes[:, w, j * P : (j + 1) * P],
                        x_words[:, 2 * half + j, w:WORDS:2],
                        row_masks[u][:, 2 * half + j, :],
                    )
            planes_of[u, half] = planes

        def group(u, half):
            if u not in groups:
                grouped = work.tile([P, 4 * BLOCK], BF16, name="grouped", align_bytes=64)
                groups[u] = grouped
            grouped_words = groups[u][:].bitcast(F32)
            nc.scalar.copy(
                out=grouped_words[:, half * BLOCK : (half + 1) * BLOCK].rearrange("p (r w) -> p r w", w=2),
                in_=planes_of[u, half][:].rearrange("p w r -> p r w"),
            )

        def quantise(u):
            x_codes = work.tile([P, BLOCK], U32, name="x_codes", align_bytes=64)
            x_scales = work.tile([P, BLOCK], U8, name="x_scales", align_bytes=64)
            nc.vector.quantize_mx(out=x_codes[:].bitcast(FP8X4), scales=x_scales[:], in_=groups[u][:])
            quantised[u] = (x_codes, x_scales)

        def multiply(u, c):
            x_codes, x_scales = quantised[u]
            acc = acc_psum.tile([P, BLOCK], F32, name="acc")
            nc.tensor.matmul_mx(
                out=acc[:],
                lhsT=w_words[:, 2 * c * P : 2 * (c + 1) * P].bitcast(FP4X4),
                lhsT_scale=w_scales[:, c * P : (c + 1) * P],
                rhs=x_codes[:].bitcast(FP8X4),
                rhs_scale=x_scales[:],
                start=True,
                stop=True,
            )
            sums[c] = acc

        def activate(u, c):
            y = y_pool.tile([P, BLOCK], F32, name="y")
            nc.scalar.activation(out=y[:], in_=sums[c][:], func=ACT.Gelu, bias=b_col[:, c : c + 1])
            outputs[c] = y

        def take_stats(u, c, pairs):
            for pair in pairs:
                s = u * BLOCK_SAMPLES + 2 * pair
                nc.vector.bn_stats(
                    out=stats[:, c, :, s : s + 2].rearrange("p v s -> p s v"),
                    in_=outputs[c][:].rearrange("p (i q j) -> p i j q", i=TILES, q=BLOCK_SAMPLES)[
                        :, :, :, 2 * pair : 2 * pair + 2
                    ],
                )

        valid = const.tile([P, NTILES], F32)
        valid_rows = const.tile([P, NBLOCKS], F32)
        spread = const.tile([P, NBLOCKS, BLOCK_SAMPLES], BF16)
        pad_y_col = const.tile([P, CHUNKS], F32)
        pad_y_diag = const.tile([P, CHUNKS, P], F32)

        def find_pad_y():
            nc.scalar.activation(out=pad_y_col[:], in_=b_col[:], func=ACT.Gelu)

        def lay_out_pad_y():
            for c in range(CHUNKS):
                nc.gpsimd.tensor_scalar(
                    out=pad_y_diag[:, c, :], in0=ident[:], scalar1=pad_y_col[:, c : c + 1], scalar2=0.0, op0=ALU.mult, op1=ALU.add
                )

        def mark_valid_rows():
            nc.gpsimd.tensor_scalar(
                out=valid[:], in0=any_differs[:], scalar1=0.0, scalar2=1.0, op0=ALU.is_gt, op1=ALU.mult
            )
            nc.vector.tensor_reduce(
                out=valid_rows[:],
                in_=valid[:].rearrange("p (u i) -> p u i", i=TILES),
                axis=mybir.AxisListType.X,
                op=ALU.add,
            )
            nc.gpsimd.tensor_tensor(
                out=spread[:],
                in0=valid_rows[:].unsqueeze(2).to_broadcast([P, NBLOCKS, BLOCK_SAMPLES]),
                in1=owner[:].unsqueeze(1).to_broadcast([P, NBLOCKS, BLOCK_SAMPLES]),
                op=ALU.mult,
            )

        stretch = const.tile([P, 1], F32)
        between = const.tile([P, 1], F32)
        scale_var = const.tile([P, 1], F32)
        pad_y_some = const.tile([P, OUT], F32)

        def count_valid_rows():
            n_ps = flip_psum.tile([P, NARROW], F32, tag="planes")
            nc.tensor.matmul(
                out=n_ps[:], lhsT=spread[:].rearrange("p u q -> p (u q)"), rhs=ones[:], start=True, stop=True
            )
            pad_y_ps = flip_psum.tile([P, OUT], F32, tag="planes")
            for c in range(CHUNKS):
                nc.tensor.transpose(
                    pad_y_ps[:, c * P : (c + 1) * P], pad_y_col[:, c : c + 1].to_broadcast([P, P]), ident[:]
                )
            return n_ps, pad_y_ps

        def derive_counts(n_ps, pad_y_ps):
            n = const.tile([P, 1], F32)
            nc.scalar.copy(out=n[:], in_=n_ps[:, 0:1])
            some = const.tile([P, 1], F32)
            nc.gpsimd.tensor_scalar(out=some[:], in0=n[:], scalar1=1.0, scalar2=1.0, op0=ALU.min, op1=ALU.mult)
            at_least_1 = const.tile([P, 1], F32)
            nc.gpsimd.tensor_scalar(out=at_least_1[:], in0=n[:], scalar1=1.0, scalar2=1.0, op0=ALU.max, op1=ALU.mult)
            dof = const.tile([P, 1], F32)
            nc.gpsimd.tensor_scalar(out=dof[:], in0=n[:], scalar1=-1.0, scalar2=1.0, op0=ALU.add, op1=ALU.max)
            padding = const.tile([P, 1], F32)
            nc.gpsimd.tensor_scalar(
                out=padding[:], in0=n[:], scalar1=-float(TOKENS), scalar2=float(TOKENS), op0=ALU.add, op1=ALU.mult
            )
            return pad_y_ps, n, some, at_least_1, dof, padding

        def invert_counts(pad_y_ps, n, some, at_least_1, dof, padding):
            inv_n = const.tile([P, 1], F32)
            nc.vector.reciprocal(out=inv_n[:], in_=at_least_1[:])
            inv_dof = const.tile([P, 1], F32)
            nc.vector.reciprocal(out=inv_dof[:], in_=dof[:])
            nc.gpsimd.tensor_scalar(
                out=stretch[:], in0=inv_n[:], scalar1=float(TOKENS), scalar2=some[:, 0:1], op0=ALU.mult, op1=ALU.mult
            )
            nc.gpsimd.tensor_tensor(out=between[:], in0=padding[:], in1=inv_n[:], op=ALU.mult)
            nc.gpsimd.tensor_scalar(
                out=scale_var[:], in0=n[:], scalar1=1.0, scalar2=inv_dof[:, 0:1], op0=ALU.is_gt, op1=ALU.mult
            )
            return pad_y_ps, some

        def spread_pad_y(pad_y_ps, some):
            nc.scalar.activation(out=pad_y_some[:], in_=pad_y_ps[:], func=ACT.Copy, scale=some[:, 0:1])

        turned = {}
        m32_turned = {}
        squares = {}
        withins = {}
        result = const.tile([P, 2 * OUT], F32)

        def open_chunk(c):
            d_t = acc_psum.tile([P, P], F32, tag="acc")
            nc.tensor.matmul(out=d_t[:], lhsT=minus_ones[:], rhs=pad_y_diag[:, c, :], start=True, stop=False)
            turned[c] = d_t

        def turn_chunk(c):
            nc.tensor.matmul(out=turned[c][:], lhsT=stats[:, c, 1, :], rhs=ident[:], start=False, stop=True)
            m32_t = flip_psum.tile([P, P], F32, tag="planes")
            nc.tensor.transpose(m32_t[:], stats[:, c, 2, :], ident[:])
            m32_turned[c] = m32_t

        def square_chunk(c):
            square = ends.tile([P, P], F32, name="square")
            nc.scalar.activation(out=square[:], in_=turned[c][:], func=ACT.Square)
            squares[c] = square

        def finish_mean(c):
            nc.vector.scalar_tensor_tensor(
                out=result[:, OUT + c * P : OUT + (c + 1) * P],
                in0=turned[c][:],
                scalar=stretch[:, 0:1],
                in1=pad_y_some[:, c * P : (c + 1) * P],
                op0=ALU.mult,
                op1=ALU.add,
            )

        def finish_sum(c):
            within = ends.tile([P, P], F32, name="within")
            nc.vector.scalar_tensor_tensor(
                out=within[:],
                in0=squares[c][:],
                scalar=between[:, 0:1],
                in1=m32_turned[c][:],
                op0=ALU.mult,
                op1=ALU.add,
            )
            withins[c] = within

        def clip_sum(c):
            nc.vector.tensor_scalar_max(out=withins[c][:], in0=withins[c][:], scalar1=0.0)

        def root_chunk(c):
            nc.scalar.activation(
                out=result[:, c * P : (c + 1) * P], in_=withins[c][:], func=ACT.Sqrt, scale=scale_var[:, 0:1]
            )

        all_pairs = range(PAIRS)
        front, back = range(PAIRS // 2), range(PAIRS // 2, PAIRS)

        def scalar_tests(u):
            for i in range(vector_tests(u), TILES):
                test_on_scalar(u, i)

        def test_on_both(u):
            flag_words(u)
            for i in range(vector_tests(u), TILES):
                test_on_scalar(u, i)
            join_flags(u)

        test_on_both(0)
        make_masks(0, range(2))
        flip(0, 0)
        make_masks(0, range(2, TILES))
        flip(0, 1)
        test_on_both(1)
        group(0, 0)
        scalar_tests(2)
        flag_words(2)
        make_masks(1, range(TILES))
        flip(1, 0)
        flip(1, 1)
        group(0, 1)
        join_flags(2)
        flag_words(3)
        scalar_tests(3)
        make_masks(2, range(TILES))
        join_flags(3)
        quantise(0)
        group(1, 0)
        place_bias()
        flag_words(4)
        make_masks(3, range(TILES))
        join_flags(4)
        multiply(0, 0)
        multiply(0, 1)
        flip(2, 0)
        flip(2, 1)
        multiply(0, 2)
        multiply(0, 3)
        scalar_tests(4)
        group(1, 1)
        find_pad_y()

        for u in range(NBLOCKS - 1):
            nxt, copied, turn, mask, test = u + 1, u + 2, u + 3, u + 4, u + AHEAD
            if u == 0:
                flag_words(test)
            quantise(nxt)
            if 0 < u and test < NBLOCKS:
                flag_words(test)
            activate(u, 0)
            if 0 < u and copied < NBLOCKS:
                group(copied, 0)
            take_stats(u, 0, front)
            if test < NBLOCKS:
                join_flags(test)
            take_stats(u, 0, back)
            multiply(nxt, 0)
            if turn < NBLOCKS:
                flip(turn, 0)
                flip(turn, 1)
            activate(u, 1)
            if u == 0:
                group(copied, 0)
            if copied < NBLOCKS:
                group(copied, 1)
            take_stats(u, 1, front)
            if mask < NBLOCKS:
                make_masks(mask, range(TILES))
            take_stats(u, 1, back)
            multiply(nxt, 1)
            if u == NBLOCKS - 3:
                count_banks = count_valid_rows()
            activate(u, 2)
            if test < NBLOCKS:
                for i in range(vector_tests(test), TILES - 1):
                    test_on_scalar(test, i)
            take_stats(u, 2, all_pairs)
            multiply(nxt, 2)
            activate(u, 3)
            if test < NBLOCKS and vector_tests(test) < TILES:
                test_on_scalar(test, 3)
            take_stats(u, 3, all_pairs)
            multiply(nxt, 3)
            if u == NBLOCKS - 4:
                mark_valid_rows()
                lay_out_pad_y()
            if u == NBLOCKS - 3:
                counts = derive_counts(*count_banks)

        u = NBLOCKS - 1
        pads = invert_counts(*counts)
        for c in range(CHUNKS):
            activate(u, c)
        nc.scalar.activation(out=warm[:], in_=one[:], func=ACT.Sqrt)
        for c in range(CHUNKS):
            open_chunk(c)
        for c in range(CHUNKS - 1):
            take_stats(u, c, all_pairs)
            turn_chunk(c)
            square_chunk(c)
            if c == 1:
                spread_pad_y(*pads)
        take_stats(u, CHUNKS - 1, all_pairs)
        turn_chunk(CHUNKS - 1)
        finish_sum(0)
        finish_sum(1)
        clip_sum(0)
        finish_sum(2)
        clip_sum(1)
        square_chunk(3)
        clip_sum(2)
        root_chunk(0)
        root_chunk(1)
        root_chunk(2)
        finish_mean(0)
        finish_mean(1)
        finish_sum(3)
        finish_mean(2)
        clip_sum(3)
        finish_mean(3)
        nc.sync.dma_start(out=out[:, OUT : OUT + 2 * P], in_=result[:, OUT : OUT + 2 * P])
        nc.sync.dma_start(out=out[:, 0 : 3 * P], in_=result[:, 0 : 3 * P])
        nc.sync.dma_start(out=out[:, OUT + 2 * P : OUT + 3 * P], in_=result[:, OUT + 2 * P : OUT + 3 * P])
        nc.sync.dma_start(out=out[:, OUT + 3 * P : 2 * OUT], in_=result[:, OUT + 3 * P : 2 * OUT])
        root_chunk(3)
        nc.scalar.dma_start(out=out[:, 3 * P : OUT], in_=result[:, 3 * P : OUT])
